import numpy as np
import ml_dtypes


def mxq(x, axis, fmt="e4m3"):
    dtype, down = {"e4m3": (ml_dtypes.float8_e4m3fn, 7), "e5m2": (ml_dtypes.float8_e5m2, 14)}[fmt]
    v = np.moveaxis(np.asarray(x, np.float32).astype(ml_dtypes.bfloat16).astype(np.float64), axis, -1)
    blocks = v.reshape(v.shape[:-1] + (-1, 32))
    amax = np.abs(blocks).max(-1, keepdims=True)
    byte = np.maximum(np.where(amax > 0, np.frexp(amax)[1] - 1 + 127, 0) - down, 1)
    scale = np.exp2(byte - 127.0)
    codes = (blocks / scale).astype(np.float32).astype(dtype).astype(np.float64)
    return np.moveaxis((codes * scale).reshape(v.shape), -1, axis)


WIDE = False


def mx_kscale(k):
    if not WIDE:
        return np.ones(k)
    levels = np.array([10, -10, 5, -5, 0])
    a = np.random.permutation(np.resize(levels, k // 512 * 4)).reshape(k // 512, 4)
    idx = np.arange(k)
    return np.exp2(a[idx // 512, idx % 128 // 32])


BF16 = ml_dtypes.bfloat16


def bf(x):
    return np.asarray(x, np.float32).astype(BF16)


def f64(x):
    return np.asarray(x).astype(np.float64)


NX, NTEST, DX, DY = 512, 8192, 256, 256
L_MEAN = 8.0
DM = DX + DY
SIG = 2.0 * L_MEAN / np.sqrt(DM)
ZS = np.exp(4.0) / np.sqrt(NX)


def setup_inputs():
    s = mx_kscale(NX)
    return {"x_mu": bf(np.random.standard_normal((NTEST, DX)) * SIG),
            "y_mean": bf(np.random.standard_normal((NTEST, DY)) * SIG),
            "y_var": bf(np.random.standard_normal((NTEST, DY)) * 0.5 * SIG),
            "X_mean": bf(np.random.standard_normal((NX, DM)) * SIG),
            "Z_mean": bf(np.random.standard_normal((NX, DY)) * ZS / s[:, None]),
            "kXXmean_inv": bf(np.random.standard_normal((NX, NX)) / np.sqrt(NX) * s)}


def reference(x_mu, y_mean, y_var, X_mean, Z_mean, kXXmean_inv):
    X = f64(X_mean)
    x_mean = np.concatenate([f64(x_mu), f64(y_mean) + f64(y_var)], axis=1)
    lam = mxq(f64(kXXmean_inv), 1, "e4m3") @ mxq(f64(Z_mean), 0, "e4m3")
    cross = mxq(X, 1, "e4m3") @ mxq(x_mean, 1, "e4m3").T
    d2 = np.sum(X * X, axis=1)[:, None] + np.sum(x_mean * x_mean, axis=1)[None, :] - 2.0 * cross
    k = np.exp(-np.maximum(d2, 0.0) / (2.0 * L_MEAN * L_MEAN))
    z_mean = mxq(k, 0, "e4m3").T @ mxq(lam, 0, "e4m3")
    return f64(y_mean) + z_mean

@@ -1,0 +1,269 @@
+from contextlib import ExitStack
+
+import concourse.mybir as mybir
+from concourse.masks import make_identity
+
+F32 = mybir.dt.float32
+BF16 = mybir.dt.bfloat16
+U32 = mybir.dt.uint32
+U8 = mybir.dt.uint8
+FP8X4 = mybir.dt.float8_e4m3fn_x4
+ALU = mybir.AluOpType
+ACT = mybir.ActivationFunctionType
+
+P = 128
+PACK = 4
+NX = 512
+NTEST = 8192
+DX = 256
+DY = 256
+DM = DX + DY
+CHUNK = 512
+TILES = CHUNK // P
+N_CHUNKS = NTEST // CHUNK
+HALF = 2 * P
+STAGES = 4
+
+FLOPS = 2 * (NX * NX * DY + NX * DM * NTEST + NTEST * NX * DY)
+
+
+def transpose_words_and_quantise(nc, pools, ident, word_block, codes, scales):
+    grouped = pools["work"].tile([P, CHUNK, PACK], BF16, align_bytes=64, name="grouped")
+    grouped_words = grouped[:].bitcast(F32)
+    for b in range(CHUNK // HALF):
+        planes = pools["planes"].tile([P, 2, HALF], F32, name="planes")
+        for a in range(HALF // P):
+            for u in range(2):
+                nc.tensor.transpose(
+                    out=planes[:, u, a * P : (a + 1) * P],
+                    in_=word_block(b * (HALF // P) + a, u),
+                    identity=ident[:],
+                )
+        nc.scalar.copy(
+            out=grouped_words[:, b * HALF : (b + 1) * HALF, :],
+            in_=planes[:].rearrange("p u n -> p n u"),
+        )
+    nc.vector.quantize_mx(
+        out=codes.bitcast(FP8X4),
+        scales=scales,
+        in_=grouped[:].rearrange("p n t -> p (n t)"),
+    )
+
+
+def mx_tiles(pool, width, name):
+    codes = pool.tile([P, width], U32, align_bytes=64, name=name + "_codes")
+    scales = pool.tile([P, width], U8, align_bytes=64, name=name + "_scales")
+    return codes, scales
+
+
+def tile_condtransportkernel_pa_t_kernel(
+    tc, x_mu, y_mean, y_var, X_mean, Z_mean, kXXmean_inv, out
+):
+    nc = tc.nc
+    with ExitStack() as stack:
+        pools = {
+            "const": stack.enter_context(tc.tile_pool(name="const", bufs=1)),
+            "loads": stack.enter_context(tc.tile_pool(name="loads", bufs=4)),
+            "y_mean": stack.enter_context(tc.tile_pool(name="y_mean", bufs=STAGES + 2)),
+            "work": stack.enter_context(tc.tile_pool(name="work", bufs=2)),
+            "planes": stack.enter_context(tc.psum_pool(name="planes", bufs=2)),
+            "spread": stack.enter_context(tc.psum_pool(name="spread", bufs=1)),
+            "cross": stack.enter_context(tc.psum_pool(name="cross", bufs=3)),
+            "product": stack.enter_context(tc.psum_pool(name="product", bufs=2)),
+        }
+        const = pools["const"]
+        work = pools["work"]
+
+        ident = const.tile([P, P], F32, name="ident")
+        make_identity(nc, ident[:])
+
+        def load_chunk(g):
+            rows = slice(g * CHUNK, (g + 1) * CHUNK)
+            xm = pools["loads"].tile([P, TILES, DX], BF16, name="xm")
+            ym = pools["y_mean"].tile([P, TILES, DY], BF16, name="ym")
+            yv = pools["loads"].tile([P, TILES, DY], BF16, name="yv")
+            for tile_, source in ((xm, x_mu), (ym, y_mean), (yv, y_var)):
+                nc.sync.dma_start(
+                    out=tile_[:], in_=source[rows, :].rearrange("(p a) c -> p a c", a=TILES)
+                )
+            return {"xm": xm, "ym": ym, "yv": yv}
+
+        x_train = const.tile([P, PACK, DM], BF16, name="x_train")
+        nc.sync.dma_start(out=x_train[:], in_=X_mean.rearrange("(p t) c -> p t c", t=PACK))
+        chunks = {0: load_chunk(0)}
+        k_inv = const.tile([P, PACK, NX], BF16, name="k_inv")
+        nc.sync.dma_start(out=k_inv[:], in_=kXXmean_inv.rearrange("(p t) c -> p t c", t=PACK))
+        z_rows = const.tile([P, PACK, DY], BF16, name="z_rows")
+        for u in range(2):
+            nc.sync.dma_start(
+                out=z_rows[:, 2 * u : 2 * u + 2, :],
+                in_=Z_mean[u * HALF : (u + 1) * HALF, :].rearrange("(q e) d -> q e d", e=2),
+            )
+
+        squares_x = const.tile([P, PACK, DM], BF16, name="squares_x")
+        sx = const.tile([P, PACK], F32, name="sx")
+        for t in range(PACK):
+            nc.scalar.activation(
+                out=squares_x[:, t, :], in_=x_train[:, t, :], func=ACT.Square,
+                accum_out=sx[:, t : t + 1],
+            )
+        half_sx = const.tile([P, PACK], F32, name="half_sx")
+        nc.scalar.mul(out=half_sx[:], in_=sx[:], mul=0.5)
+
+        x_train_words = x_train[:].bitcast(F32)
+        xt_codes, xt_scales = mx_tiles(const, NX, "xt")
+        transpose_words_and_quantise(
+            nc, pools, ident,
+            lambda t, u: x_train_words[:, t, u * P : (u + 1) * P],
+            xt_codes[:], xt_scales[:],
+        )
+
+        def make_lam():
+            k_inv_words = k_inv[:].bitcast(F32)
+            ki_codes, ki_scales = mx_tiles(const, NX, "ki")
+            transpose_words_and_quantise(
+                nc, pools, ident,
+                lambda t, u: k_inv_words[:, t, u * P : (u + 1) * P],
+                ki_codes[:], ki_scales[:],
+            )
+            z_grouped = const.tile([P, DY, PACK], BF16, align_bytes=64, name="z_grouped")
+            nc.vector.tensor_copy(out=z_grouped[:], in_=z_rows[:].rearrange("p t d -> p d t"))
+            z_codes, z_scales = mx_tiles(const, DY, "z")
+            nc.vector.quantize_mx(
+                out=z_codes[:].bitcast(FP8X4), scales=z_scales[:],
+                in_=z_grouped[:].rearrange("p d t -> p (d t)"),
+            )
+            lam_grouped = const.tile([P, DY, PACK], BF16, align_bytes=64, name="lam_grouped")
+            for b in range(2):
+                lam_psum = pools["product"].tile([P, 2, DY], F32, name="product")
+                for t in (2 * b, 2 * b + 1):
+                    nc.tensor.matmul_mx(
+                        out=lam_psum[:, t - 2 * b, :],
+                        lhsT=ki_codes[:, t * P : (t + 1) * P].bitcast(FP8X4),
+                        lhsT_scale=ki_scales[:, t * P : (t + 1) * P],
+                        rhs=z_codes[:].bitcast(FP8X4),
+                        rhs_scale=z_scales[:],
+                        start=True, stop=True,
+                    )
+                nc.vector.tensor_copy(
+                    out=lam_grouped[:, :, 2 * b : 2 * b + 2],
+                    in_=lam_psum[:].rearrange("p t d -> p d t"),
+                )
+            lam_codes, lam_scales = mx_tiles(const, DY, "lam")
+            nc.vector.quantize_mx(
+                out=lam_codes[:].bitcast(FP8X4), scales=lam_scales[:],
+                in_=lam_grouped[:].rearrange("p d t -> p (d t)"),
+            )
+            return lam_codes, lam_scales
+
+        def prepare(c):
+            y_f32 = work.tile([P, TILES, DY], F32, name="y_f32")
+            nc.gpsimd.tensor_tensor(out=y_f32[:], in0=c["ym"][:], in1=c["yv"][:], op=ALU.add)
+            y_bf16 = work.tile([P, TILES, DY], BF16, name="y_bf16")
+            nc.vector.tensor_tensor(out=y_bf16[:], in0=c["ym"][:], in1=c["yv"][:], op=ALU.add)
+            squares = work.tile([P, 2 * TILES, DY], BF16, name="squares")
+            sum_x = work.tile([P, TILES], F32, name="sum_x")
+            sum_y = work.tile([P, TILES], F32, name="sum_y")
+            for a in range(TILES):
+                nc.scalar.activation(
+                    out=squares[:, 2 * a, :], in_=c["xm"][:, a, :], func=ACT.Square,
+                    accum_out=sum_x[:, a : a + 1],
+                )
+                nc.scalar.activation(
+                    out=squares[:, 2 * a + 1, :], in_=y_f32[:, a, :], func=ACT.Square,
+                    accum_out=sum_y[:, a : a + 1],
+                )
+            repeated = work.tile([P, TILES, P], F32, name="repeated")
+            nc.gpsimd.tensor_tensor(
+                out=repeated[:],
+                in0=sum_x[:].unsqueeze(2).to_broadcast([P, TILES, P]),
+                in1=sum_y[:].unsqueeze(2).to_broadcast([P, TILES, P]),
+                op=ALU.add,
+            )
+            c["y_bf16"] = y_bf16
+            c["repeated"] = repeated
+
+        def transpose(c):
+            xm_words = c["xm"][:].bitcast(F32)
+            y_words = c["y_bf16"][:].bitcast(F32)
+            q_codes, q_scales = mx_tiles(work, CHUNK, "q")
+            transpose_words_and_quantise(
+                nc, pools, ident,
+                lambda a, u: (xm_words, y_words)[u][:, a, :],
+                q_codes[:], q_scales[:],
+            )
+            spread = pools["spread"].tile([P, TILES, P], F32, name="spread")
+            for a in range(TILES):
+                nc.tensor.transpose(
+                    out=spread[:, a, :], in_=c["repeated"][:, a, :], identity=ident[:]
+                )
+            half_sq = work.tile([P, CHUNK], F32, name="half_sq")
+            nc.scalar.mul(out=half_sq[:], in_=spread[:].rearrange("p a r -> p (a r)"), mul=0.5)
+            c["q_codes"], c["q_scales"], c["half_sq"] = q_codes, q_scales, half_sq
+
+        def kernel(c):
+            minus_half_d2 = work.tile([P, PACK, CHUNK], F32, name="minus_half_d2")
+            for t in range(PACK):
+                cross = pools["cross"].tile([P, CHUNK], F32, name="cross")
+                nc.tensor.matmul_mx(
+                    out=cross[:],
+                    lhsT=xt_codes[:, t * P : (t + 1) * P].bitcast(FP8X4),
+                    lhsT_scale=xt_scales[:, t * P : (t + 1) * P],
+                    rhs=c["q_codes"][:].bitcast(FP8X4),
+                    rhs_scale=c["q_scales"][:],
+                    start=True, stop=True,
+                )
+                nc.vector.scalar_tensor_tensor(
+                    out=minus_half_d2[:, t, :], in0=cross[:], scalar=half_sx[:, t : t + 1],
+                    in1=c["half_sq"][:], op0=ALU.subtract, op1=ALU.subtract,
+                )
+            unclamped = work.tile([P, PACK, CHUNK], BF16, name="unclamped")
+            nc.scalar.activation(
+                out=unclamped[:], in_=minus_half_d2[:], func=ACT.Exp, scale=1.0 / 64.0
+            )
+            c["unclamped"] = unclamped
+
+        def finish(g, c, lam_codes, lam_scales):
+            k_grouped = work.tile([P, CHUNK, PACK], BF16, align_bytes=64, name="k_grouped")
+            nc.vector.tensor_scalar(
+                out=k_grouped[:], in0=c["unclamped"][:].rearrange("p t n -> p n t"),
+                scalar1=1.0, scalar2=None, op0=ALU.min,
+            )
+            k_codes, k_scales = mx_tiles(work, CHUNK, "k")
+            nc.vector.quantize_mx(
+                out=k_codes[:].bitcast(FP8X4), scales=k_scales[:],
+                in_=k_grouped[:].rearrange("p n t -> p (n t)"),
+            )
+            result = work.tile([P, TILES, DY], F32, name="result")
+            for b in range(TILES // 2):
+                product = pools["product"].tile([P, 2, DY], F32, name="product")
+                for a in (2 * b, 2 * b + 1):
+                    nc.tensor.matmul_mx(
+                        out=product[:, a - 2 * b, :],
+                        lhsT=k_codes[:, a * P : (a + 1) * P].bitcast(FP8X4),
+                        lhsT_scale=k_scales[:, a * P : (a + 1) * P],
+                        rhs=lam_codes[:].bitcast(FP8X4),
+                        rhs_scale=lam_scales[:],
+                        start=True, stop=True,
+                    )
+                nc.vector.tensor_tensor(
+                    out=result[:, 2 * b : 2 * b + 2, :], in0=product[:],
+                    in1=c["ym"][:, 2 * b : 2 * b + 2, :], op=ALU.add,
+                )
+            nc.sync.dma_start(
+                out=out[g * CHUNK : (g + 1) * CHUNK, :].rearrange("(p a) d -> p a d", a=TILES),
+                in_=result[:],
+            )
+
+        lam_codes, lam_scales = make_lam()
+        for step in range(N_CHUNKS + STAGES - 1):
+            if step + 1 < N_CHUNKS:
+                chunks[step + 1] = load_chunk(step + 1)
+            if 0 <= step - 3:
+                finish(step - 3, chunks[step - 3], lam_codes, lam_scales)
+            if 0 <= step - 2 < N_CHUNKS:
+                kernel(chunks[step - 2])
+            if 0 <= step - 1 < N_CHUNKS:
+                transpose(chunks[step - 1])
+            if step < N_CHUNKS:
+                prepare(chunks[step])

@@ -22,12 +22,18 @@ CHUNK = 512
 TILES = CHUNK // P
 N_CHUNKS = NTEST // CHUNK
 HALF = 2 * P
-STAGES = 4
+STAGES = 5
 
 FLOPS = 2 * (NX * NX * DY + NX * DM * NTEST + NTEST * NX * DY)
 
 
-def transpose_words_and_quantise(nc, pools, ident, word_block, codes, scales):
+def mx_tiles(pool, width, name):
+    codes = pool.tile([P, width], U32, align_bytes=64, name=name + "_codes")
+    scales = pool.tile([P, width], U8, align_bytes=64, name=name + "_scales")
+    return codes, scales
+
+
+def transpose_words_and_quantise(nc, pools, ident, word_block, name):
     grouped = pools["work"].tile([P, CHUNK, PACK], BF16, align_bytes=64, name="grouped")
     grouped_words = grouped[:].bitcast(F32)
     for b in range(CHUNK // HALF):
@@ -43,16 +49,12 @@ def transpose_words_and_quantise(nc, pools, ident, word_block, codes, scales):
             out=grouped_words[:, b * HALF : (b + 1) * HALF, :],
             in_=planes[:].rearrange("p u n -> p n u"),
         )
+    codes, scales = mx_tiles(pools[name], CHUNK, name)
     nc.vector.quantize_mx(
-        out=codes.bitcast(FP8X4),
-        scales=scales,
+        out=codes[:].bitcast(FP8X4),
+        scales=scales[:],
         in_=grouped[:].rearrange("p n t -> p (n t)"),
     )
-
-
-def mx_tiles(pool, width, name):
-    codes = pool.tile([P, width], U32, align_bytes=64, name=name + "_codes")
-    scales = pool.tile([P, width], U8, align_bytes=64, name=name + "_scales")
     return codes, scales
 
 
@@ -61,18 +63,17 @@ def tile_condtransportkernel_pa_t_kernel(
 ):
     nc = tc.nc
     with ExitStack() as stack:
+        const = stack.enter_context(tc.tile_pool(name="const", bufs=1))
+        work = stack.enter_context(tc.tile_pool(name="work", bufs=3))
         pools = {
-            "const": stack.enter_context(tc.tile_pool(name="const", bufs=1)),
+            "work": work,
+            "x_train": const, "k_inv": const, "query": work, "kernel": work,
             "loads": stack.enter_context(tc.tile_pool(name="loads", bufs=4)),
             "y_mean": stack.enter_context(tc.tile_pool(name="y_mean", bufs=STAGES + 2)),
-            "work": stack.enter_context(tc.tile_pool(name="work", bufs=2)),
-            "planes": stack.enter_context(tc.psum_pool(name="planes", bufs=2)),
-            "spread": stack.enter_context(tc.psum_pool(name="spread", bufs=1)),
+            "planes": stack.enter_context(tc.psum_pool(name="planes", bufs=3)),
             "cross": stack.enter_context(tc.psum_pool(name="cross", bufs=3)),
             "product": stack.enter_context(tc.psum_pool(name="product", bufs=2)),
         }
-        const = pools["const"]
-        work = pools["work"]
 
         ident = const.tile([P, P], F32, name="ident")
         make_identity(nc, ident[:])
@@ -88,43 +89,51 @@ def tile_condtransportkernel_pa_t_kernel(
                 )
             return {"xm": xm, "ym": ym, "yv": yv}
 
-        x_train = const.tile([P, PACK, DM], BF16, name="x_train")
-        nc.sync.dma_start(out=x_train[:], in_=X_mean.rearrange("(p t) c -> p t c", t=PACK))
-        chunks = {0: load_chunk(0)}
-        k_inv = const.tile([P, PACK, NX], BF16, name="k_inv")
-        nc.sync.dma_start(out=k_inv[:], in_=kXXmean_inv.rearrange("(p t) c -> p t c", t=PACK))
-        z_rows = const.tile([P, PACK, DY], BF16, name="z_rows")
-        for u in range(2):
-            nc.sync.dma_start(
-                out=z_rows[:, 2 * u : 2 * u + 2, :],
-                in_=Z_mean[u * HALF : (u + 1) * HALF, :].rearrange("(q e) d -> q e d", e=2),
-            )
+        def load_in_word_order(source, width, name):
+            rows = const.tile([P, PACK, width], BF16, name=name)
+            for u in range(2):
+                nc.sync.dma_start(
+                    out=rows[:, 2 * u : 2 * u + 2, :],
+                    in_=source[u * HALF : (u + 1) * HALF, :].rearrange("(q e) c -> q e c", e=2),
+                )
+            return rows
 
-        squares_x = const.tile([P, PACK, DM], BF16, name="squares_x")
-        sx = const.tile([P, PACK], F32, name="sx")
-        for t in range(PACK):
-            nc.scalar.activation(
-                out=squares_x[:, t, :], in_=x_train[:, t, :], func=ACT.Square,
-                accum_out=sx[:, t : t + 1],
-            )
-        half_sx = const.tile([P, PACK], F32, name="half_sx")
-        nc.scalar.mul(out=half_sx[:], in_=sx[:], mul=0.5)
+        x_train = const.tile([P, TILES, DM], BF16, name="x_train")
+        nc.sync.dma_start(out=x_train[:], in_=X_mean.rearrange("(t p) c -> p t c", p=P))
+        chunks = {0: load_chunk(0)}
+        k_inv = load_in_word_order(kXXmean_inv, NX, "k_inv")
+        z_rows = load_in_word_order(Z_mean, DY, "z_rows")
 
         x_train_words = x_train[:].bitcast(F32)
-        xt_codes, xt_scales = mx_tiles(const, NX, "xt")
-        transpose_words_and_quantise(
-            nc, pools, ident,
-            lambda t, u: x_train_words[:, t, u * P : (u + 1) * P],
-            xt_codes[:], xt_scales[:],
+        xt_codes, xt_scales = transpose_words_and_quantise(
+            nc, pools, ident, lambda t, u: x_train_words[:, t, u * P : (u + 1) * P], "x_train"
         )
+
+        def spread_half_sx():
+            squares_x = const.tile([P, TILES, DM], BF16, name="squares_x")
+            sx = const.tile([P, TILES], F32, name="sx")
+            for t in range(TILES):
+                nc.scalar.activation(
+                    out=squares_x[:, t, :], in_=x_train[:, t, :], func=ACT.Square,
+                    accum_out=sx[:, t : t + 1],
+                )
+            repeated = const.tile([P, TILES, P], F32, name="repeated")
+            nc.vector.tensor_copy(
+                out=repeated[:], in_=sx[:].unsqueeze(2).to_broadcast([P, TILES, P])
+            )
+            spread = pools["cross"].tile([P, NX], F32, name="cross")
+            for t in range(TILES):
+                nc.tensor.transpose(
+                    out=spread[:, t * P : (t + 1) * P], in_=repeated[:, t, :], identity=ident[:]
+                )
+            half_sx = const.tile([P, NX], F32, name="half_sx")
+            nc.scalar.mul(out=half_sx[:], in_=spread[:], mul=0.5)
+            return half_sx
 
         def make_lam():
             k_inv_words = k_inv[:].bitcast(F32)
-            ki_codes, ki_scales = mx_tiles(const, NX, "ki")
-            transpose_words_and_quantise(
-                nc, pools, ident,
-                lambda t, u: k_inv_words[:, t, u * P : (u + 1) * P],
-                ki_codes[:], ki_scales[:],
+            ki_codes, ki_scales = transpose_words_and_quantise(
+                nc, pools, ident, lambda t, u: k_inv_words[:, t, u * P : (u + 1) * P], "k_inv"
             )
             z_grouped = const.tile([P, DY, PACK], BF16, align_bytes=64, name="z_grouped")
             nc.vector.tensor_copy(out=z_grouped[:], in_=z_rows[:].rearrange("p t d -> p d t"))
@@ -134,11 +143,12 @@ def tile_condtransportkernel_pa_t_kernel(
                 in_=z_grouped[:].rearrange("p d t -> p (d t)"),
             )
             lam_grouped = const.tile([P, DY, PACK], BF16, align_bytes=64, name="lam_grouped")
-            for b in range(2):
+            for u in range(2):
                 lam_psum = pools["product"].tile([P, 2, DY], F32, name="product")
-                for t in (2 * b, 2 * b + 1):
+                for e in range(2):
+                    t = 2 * u + e
                     nc.tensor.matmul_mx(
-                        out=lam_psum[:, t - 2 * b, :],
+                        out=lam_psum[:, e, :],
                         lhsT=ki_codes[:, t * P : (t + 1) * P].bitcast(FP8X4),
                         lhsT_scale=ki_scales[:, t * P : (t + 1) * P],
                         rhs=z_codes[:].bitcast(FP8X4),
@@ -146,8 +156,8 @@ def tile_condtransportkernel_pa_t_kernel(
                         start=True, stop=True,
                     )
                 nc.vector.tensor_copy(
-                    out=lam_grouped[:, :, 2 * b : 2 * b + 2],
-                    in_=lam_psum[:].rearrange("p t d -> p d t"),
+                    out=lam_grouped[:, :, 2 * u : 2 * u + 2],
+                    in_=lam_psum[:].rearrange("p e d -> p d e"),
                 )
             lam_codes, lam_scales = mx_tiles(const, DY, "lam")
             nc.vector.quantize_mx(
@@ -156,9 +166,12 @@ def tile_condtransportkernel_pa_t_kernel(
             )
             return lam_codes, lam_scales
 
+        half_sx = spread_half_sx()
+        lam_codes, lam_scales = make_lam()
+
         def prepare(c):
             y_f32 = work.tile([P, TILES, DY], F32, name="y_f32")
-            nc.gpsimd.tensor_tensor(out=y_f32[:], in0=c["ym"][:], in1=c["yv"][:], op=ALU.add)
+            nc.vector.tensor_tensor(out=y_f32[:], in0=c["ym"][:], in1=c["yv"][:], op=ALU.add)
             y_bf16 = work.tile([P, TILES, DY], BF16, name="y_bf16")
             nc.vector.tensor_tensor(out=y_bf16[:], in0=c["ym"][:], in1=c["yv"][:], op=ALU.add)
             squares = work.tile([P, 2 * TILES, DY], BF16, name="squares")
@@ -173,67 +186,56 @@ def tile_condtransportkernel_pa_t_kernel(
                     out=squares[:, 2 * a + 1, :], in_=y_f32[:, a, :], func=ACT.Square,
                     accum_out=sum_y[:, a : a + 1],
                 )
-            repeated = work.tile([P, TILES, P], F32, name="repeated")
-            nc.gpsimd.tensor_tensor(
-                out=repeated[:],
-                in0=sum_x[:].unsqueeze(2).to_broadcast([P, TILES, P]),
-                in1=sum_y[:].unsqueeze(2).to_broadcast([P, TILES, P]),
-                op=ALU.add,
+            sq = work.tile([P, TILES], F32, name="sq")
+            nc.gpsimd.tensor_tensor(out=sq[:], in0=sum_x[:], in1=sum_y[:], op=ALU.add)
+            half_sq = work.tile([P, TILES], F32, name="half_sq")
+            nc.gpsimd.tensor_scalar(
+                out=half_sq[:], in0=sq[:], scalar1=0.5, scalar2=0.0, op0=ALU.mult, op1=ALU.add
             )
-            c["y_bf16"] = y_bf16
-            c["repeated"] = repeated
+            c["y_bf16"], c["half_sq"] = y_bf16, half_sq
 
-        def transpose(c):
+        def quantise_queries(c):
             xm_words = c["xm"][:].bitcast(F32)
             y_words = c["y_bf16"][:].bitcast(F32)
-            q_codes, q_scales = mx_tiles(work, CHUNK, "q")
-            transpose_words_and_quantise(
-                nc, pools, ident,
-                lambda a, u: (xm_words, y_words)[u][:, a, :],
-                q_codes[:], q_scales[:],
+            c["query"] = transpose_words_and_quantise(
+                nc, pools, ident, lambda a, u: (xm_words, y_words)[u][:, a, :], "query"
             )
-            spread = pools["spread"].tile([P, TILES, P], F32, name="spread")
-            for a in range(TILES):
-                nc.tensor.transpose(
-                    out=spread[:, a, :], in_=c["repeated"][:, a, :], identity=ident[:]
-                )
-            half_sq = work.tile([P, CHUNK], F32, name="half_sq")
-            nc.scalar.mul(out=half_sq[:], in_=spread[:].rearrange("p a r -> p (a r)"), mul=0.5)
-            c["q_codes"], c["q_scales"], c["half_sq"] = q_codes, q_scales, half_sq
 
-        def kernel(c):
-            minus_half_d2 = work.tile([P, PACK, CHUNK], F32, name="minus_half_d2")
-            for t in range(PACK):
-                cross = pools["cross"].tile([P, CHUNK], F32, name="cross")
+        def kernel_rows(c):
+            q_codes, q_scales = c["query"]
+            minus_half_d2 = work.tile([P, TILES, NX], F32, name="minus_half_d2")
+            for a in range(TILES):
+                cross = pools["cross"].tile([P, NX], F32, name="cross")
                 nc.tensor.matmul_mx(
                     out=cross[:],
-                    lhsT=xt_codes[:, t * P : (t + 1) * P].bitcast(FP8X4),
-                    lhsT_scale=xt_scales[:, t * P : (t + 1) * P],
-                    rhs=c["q_codes"][:].bitcast(FP8X4),
-                    rhs_scale=c["q_scales"][:],
+                    lhsT=q_codes[:, a * P : (a + 1) * P].bitcast(FP8X4),
+                    lhsT_scale=q_scales[:, a * P : (a + 1) * P],
+                    rhs=xt_codes[:].bitcast(FP8X4),
+                    rhs_scale=xt_scales[:],
                     start=True, stop=True,
                 )
                 nc.vector.scalar_tensor_tensor(
-                    out=minus_half_d2[:, t, :], in0=cross[:], scalar=half_sx[:, t : t + 1],
-                    in1=c["half_sq"][:], op0=ALU.subtract, op1=ALU.subtract,
+                    out=minus_half_d2[:, a, :], in0=cross[:], scalar=c["half_sq"][:, a : a + 1],
+                    in1=half_sx[:], op0=ALU.subtract, op1=ALU.subtract,
                 )
-            unclamped = work.tile([P, PACK, CHUNK], BF16, name="unclamped")
+            k_rows = work.tile([P, TILES, NX], BF16, name="k_rows")
             nc.scalar.activation(
-                out=unclamped[:], in_=minus_half_d2[:], func=ACT.Exp, scale=1.0 / 64.0
+                out=k_rows[:], in_=minus_half_d2[:], func=ACT.Exp, scale=1.0 / 64.0
             )
-            c["unclamped"] = unclamped
+            c["k_rows"] = k_rows
 
-        def finish(g, c, lam_codes, lam_scales):
-            k_grouped = work.tile([P, CHUNK, PACK], BF16, align_bytes=64, name="k_grouped")
+        def quantise_kernel(c):
+            flat = c["k_rows"][:].rearrange("p a i -> p (a i)")
             nc.vector.tensor_scalar(
-                out=k_grouped[:], in0=c["unclamped"][:].rearrange("p t n -> p n t"),
-                scalar1=1.0, scalar2=None, op0=ALU.min,
+                out=flat, in0=flat, scalar1=1.0, scalar2=None, op0=ALU.min
             )
-            k_codes, k_scales = mx_tiles(work, CHUNK, "k")
-            nc.vector.quantize_mx(
-                out=k_codes[:].bitcast(FP8X4), scales=k_scales[:],
-                in_=k_grouped[:].rearrange("p n t -> p (n t)"),
+            k_words = c["k_rows"][:].bitcast(F32)
+            c["kernel"] = transpose_words_and_quantise(
+                nc, pools, ident, lambda a, u: k_words[:, a, u * P : (u + 1) * P], "kernel"
             )
+
+        def finish(g, c):
+            k_codes, k_scales = c["kernel"]
             result = work.tile([P, TILES, DY], F32, name="result")
             for b in range(TILES // 2):
                 product = pools["product"].tile([P, 2, DY], F32, name="product")
@@ -255,15 +257,16 @@ def tile_condtransportkernel_pa_t_kernel(
                 in_=result[:],
             )
 
-        lam_codes, lam_scales = make_lam()
         for step in range(N_CHUNKS + STAGES - 1):
             if step + 1 < N_CHUNKS:
                 chunks[step + 1] = load_chunk(step + 1)
-            if 0 <= step - 3:
-                finish(step - 3, chunks[step - 3], lam_codes, lam_scales)
+            if 0 <= step - 4:
+                finish(step - 4, chunks[step - 4])
+            if 0 <= step - 3 < N_CHUNKS:
+                quantise_kernel(chunks[step - 3])
             if 0 <= step - 2 < N_CHUNKS:
-                kernel(chunks[step - 2])
+                kernel_rows(chunks[step - 2])
             if 0 <= step - 1 < N_CHUNKS:
-                transpose(chunks[step - 1])
+                quantise_queries(chunks[step - 1])
             if step < N_CHUNKS:
                 prepare(chunks[step])

@@ -67,11 +67,12 @@ def tile_condtransportkernel_pa_t_kernel(
         work = stack.enter_context(tc.tile_pool(name="work", bufs=3))
         pools = {
             "work": work,
-            "x_train": const, "k_inv": const, "query": work, "kernel": work,
+            "x_train": const, "k_inv": const, "query": work,
             "loads": stack.enter_context(tc.tile_pool(name="loads", bufs=4)),
             "y_mean": stack.enter_context(tc.tile_pool(name="y_mean", bufs=STAGES + 2)),
-            "planes": stack.enter_context(tc.psum_pool(name="planes", bufs=3)),
-            "cross": stack.enter_context(tc.psum_pool(name="cross", bufs=3)),
+            "planes": stack.enter_context(tc.psum_pool(name="planes", bufs=2)),
+            "cross": stack.enter_context(tc.psum_pool(name="cross", bufs=2)),
+            "flipped": stack.enter_context(tc.psum_pool(name="flipped", bufs=2)),
             "product": stack.enter_context(tc.psum_pool(name="product", bufs=2)),
         }
 
@@ -89,20 +90,17 @@ def tile_condtransportkernel_pa_t_kernel(
                 )
             return {"xm": xm, "ym": ym, "yv": yv}
 
-        def load_in_word_order(source, width, name):
-            rows = const.tile([P, PACK, width], BF16, name=name)
-            for u in range(2):
-                nc.sync.dma_start(
-                    out=rows[:, 2 * u : 2 * u + 2, :],
-                    in_=source[u * HALF : (u + 1) * HALF, :].rearrange("(q e) c -> q e c", e=2),
-                )
-            return rows
-
         x_train = const.tile([P, TILES, DM], BF16, name="x_train")
         nc.sync.dma_start(out=x_train[:], in_=X_mean.rearrange("(t p) c -> p t c", p=P))
         chunks = {0: load_chunk(0)}
-        k_inv = load_in_word_order(kXXmean_inv, NX, "k_inv")
-        z_rows = load_in_word_order(Z_mean, DY, "z_rows")
+        k_inv = const.tile([P, TILES, NX], BF16, name="k_inv")
+        nc.sync.dma_start(out=k_inv[:], in_=kXXmean_inv.rearrange("(t p) c -> p t c", p=P))
+        z_rows = const.tile([P, PACK, DY], BF16, name="z_rows")
+        for u in range(2):
+            nc.sync.dma_start(
+                out=z_rows[:, 2 * u : 2 * u + 2, :],
+                in_=Z_mean[u * HALF : (u + 1) * HALF, :].rearrange("(q e) d -> q e d", e=2),
+            )
 
         x_train_words = x_train[:].bitcast(F32)
         xt_codes, xt_scales = transpose_words_and_quantise(
@@ -143,12 +141,11 @@ def tile_condtransportkernel_pa_t_kernel(
                 in_=z_grouped[:].rearrange("p d t -> p (d t)"),
             )
             lam_grouped = const.tile([P, DY, PACK], BF16, align_bytes=64, name="lam_grouped")
-            for u in range(2):
+            for b in range(2):
                 lam_psum = pools["product"].tile([P, 2, DY], F32, name="product")
-                for e in range(2):
-                    t = 2 * u + e
+                for t in (2 * b, 2 * b + 1):
                     nc.tensor.matmul_mx(
-                        out=lam_psum[:, e, :],
+                        out=lam_psum[:, t - 2 * b, :],
                         lhsT=ki_codes[:, t * P : (t + 1) * P].bitcast(FP8X4),
                         lhsT_scale=ki_scales[:, t * P : (t + 1) * P],
                         rhs=z_codes[:].bitcast(FP8X4),
@@ -156,8 +153,8 @@ def tile_condtransportkernel_pa_t_kernel(
                         start=True, stop=True,
                     )
                 nc.vector.tensor_copy(
-                    out=lam_grouped[:, :, 2 * u : 2 * u + 2],
-                    in_=lam_psum[:].rearrange("p e d -> p d e"),
+                    out=lam_grouped[:, :, 2 * b : 2 * b + 2],
+                    in_=lam_psum[:].rearrange("p t d -> p d t"),
                 )
             lam_codes, lam_scales = mx_tiles(const, DY, "lam")
             nc.vector.quantize_mx(
@@ -201,7 +198,7 @@ def tile_condtransportkernel_pa_t_kernel(
                 nc, pools, ident, lambda a, u: (xm_words, y_words)[u][:, a, :], "query"
             )
 
-        def kernel_rows(c):
+        def distances(c):
             q_codes, q_scales = c["query"]
             minus_half_d2 = work.tile([P, TILES, NX], F32, name="minus_half_d2")
             for a in range(TILES):
@@ -218,21 +215,28 @@ def tile_condtransportkernel_pa_t_kernel(
                     out=minus_half_d2[:, a, :], in0=cross[:], scalar=c["half_sq"][:, a : a + 1],
                     in1=half_sx[:], op0=ALU.subtract, op1=ALU.subtract,
                 )
-            k_rows = work.tile([P, TILES, NX], BF16, name="k_rows")
-            nc.scalar.activation(
-                out=k_rows[:], in_=minus_half_d2[:], func=ACT.Exp, scale=1.0 / 64.0
-            )
-            c["k_rows"] = k_rows
+            c["minus_half_d2"] = minus_half_d2
 
         def quantise_kernel(c):
-            flat = c["k_rows"][:].rearrange("p a i -> p (a i)")
-            nc.vector.tensor_scalar(
-                out=flat, in0=flat, scalar1=1.0, scalar2=None, op0=ALU.min
-            )
-            k_words = c["k_rows"][:].bitcast(F32)
-            c["kernel"] = transpose_words_and_quantise(
-                nc, pools, ident, lambda a, u: k_words[:, a, u * P : (u + 1) * P], "kernel"
-            )
+            k_grouped = work.tile([P, CHUNK, PACK], BF16, align_bytes=64, name="k_grouped")
+            for a in range(TILES):
+                flipped = pools["flipped"].tile([P, PACK, P], F32, name="flipped")
+                for t in range(PACK):
+                    nc.tensor.transpose(
+                        out=flipped[:, t, :],
+                        in_=c["minus_half_d2"][:, a, t * P : (t + 1) * P],
+                        identity=ident[:],
+                    )
+                nc.scalar.activation(
+                    out=k_grouped[:, a * P : (a + 1) * P, :],
+                    in_=flipped[:].rearrange("p t r -> p r t"),
+                    func=ACT.Exp, scale=1.0 / 64.0,
+                )
+            flat = k_grouped[:].rearrange("p n t -> p (n t)")
+            nc.vector.tensor_scalar(out=flat, in0=flat, scalar1=1.0, scalar2=None, op0=ALU.min)
+            k_codes, k_scales = mx_tiles(work, CHUNK, "kernel")
+            nc.vector.quantize_mx(out=k_codes[:].bitcast(FP8X4), scales=k_scales[:], in_=flat)
+            c["kernel"] = (k_codes, k_scales)
 
         def finish(g, c):
             k_codes, k_scales = c["kernel"]
@@ -265,7 +269,7 @@ def tile_condtransportkernel_pa_t_kernel(
             if 0 <= step - 3 < N_CHUNKS:
                 quantise_kernel(chunks[step - 3])
             if 0 <= step - 2 < N_CHUNKS:
-                kernel_rows(chunks[step - 2])
+                distances(chunks[step - 2])
             if 0 <= step - 1 < N_CHUNKS:
                 quantise_queries(chunks[step - 1])
             if step < N_CHUNKS:

@@ -22,7 +22,8 @@ CHUNK = 512
 TILES = CHUNK // P
 N_CHUNKS = NTEST // CHUNK
 HALF = 2 * P
-STAGES = 5
+OLDEST = 4
+AHEAD = 2
 
 FLOPS = 2 * (NX * NX * DY + NX * DM * NTEST + NTEST * NX * DY)
 
@@ -33,23 +34,8 @@ def mx_tiles(pool, width, name):
     return codes, scales
 
 
-def transpose_words_and_quantise(nc, pools, ident, word_block, name):
-    grouped = pools["work"].tile([P, CHUNK, PACK], BF16, align_bytes=64, name="grouped")
-    grouped_words = grouped[:].bitcast(F32)
-    for b in range(CHUNK // HALF):
-        planes = pools["planes"].tile([P, 2, HALF], F32, name="planes")
-        for a in range(HALF // P):
-            for u in range(2):
-                nc.tensor.transpose(
-                    out=planes[:, u, a * P : (a + 1) * P],
-                    in_=word_block(b * (HALF // P) + a, u),
-                    identity=ident[:],
-                )
-        nc.scalar.copy(
-            out=grouped_words[:, b * HALF : (b + 1) * HALF, :],
-            in_=planes[:].rearrange("p u n -> p n u"),
-        )
-    codes, scales = mx_tiles(pools[name], CHUNK, name)
+def quantise(nc, pool, grouped, name):
+    codes, scales = mx_tiles(pool, grouped.shape[1], name)
     nc.vector.quantize_mx(
         out=codes[:].bitcast(FP8X4),
         scales=scales[:],
@@ -58,18 +44,44 @@ def transpose_words_and_quantise(nc, pools, ident, word_block, name):
     return codes, scales
 
 
+def transpose_words(nc, pools, kind, ident, word_block):
+    banks = []
+    for b in range(CHUNK // HALF):
+        planes = pools[kind].tile([P, 2, HALF], F32, name=kind)
+        for a in range(HALF // P):
+            for u in range(2):
+                nc.tensor.transpose(
+                    out=planes[:, u, a * P : (a + 1) * P],
+                    in_=word_block(b * (HALF // P) + a, u),
+                    identity=ident[:],
+                )
+        banks.append(planes)
+    return banks
+
+
+def pair_words(copy, pools, banks):
+    grouped = pools["work"].tile([P, CHUNK, PACK], BF16, align_bytes=64, name="grouped")
+    grouped_words = grouped[:].bitcast(F32)
+    for b, planes in enumerate(banks):
+        copy(
+            out=grouped_words[:, b * HALF : (b + 1) * HALF, :],
+            in_=planes[:].rearrange("p u n -> p n u"),
+        )
+    return grouped
+
+
 def tile_condtransportkernel_pa_t_kernel(
     tc, x_mu, y_mean, y_var, X_mean, Z_mean, kXXmean_inv, out
 ):
     nc = tc.nc
     with ExitStack() as stack:
+        stack.enter_context(tc.manual_schedule())
         const = stack.enter_context(tc.tile_pool(name="const", bufs=1))
         work = stack.enter_context(tc.tile_pool(name="work", bufs=3))
         pools = {
             "work": work,
-            "x_train": const, "k_inv": const, "query": work,
-            "loads": stack.enter_context(tc.tile_pool(name="loads", bufs=4)),
-            "y_mean": stack.enter_context(tc.tile_pool(name="y_mean", bufs=STAGES + 2)),
+            "loads": stack.enter_context(tc.tile_pool(name="loads", bufs=AHEAD + 3)),
+            "y_mean": stack.enter_context(tc.tile_pool(name="y_mean", bufs=AHEAD + OLDEST + 2)),
             "planes": stack.enter_context(tc.psum_pool(name="planes", bufs=2)),
             "cross": stack.enter_context(tc.psum_pool(name="cross", bufs=2)),
             "flipped": stack.enter_context(tc.psum_pool(name="flipped", bufs=2)),
@@ -101,11 +113,8 @@ def tile_condtransportkernel_pa_t_kernel(
                 out=z_rows[:, 2 * u : 2 * u + 2, :],
                 in_=Z_mean[u * HALF : (u + 1) * HALF, :].rearrange("(q e) d -> q e d", e=2),
             )
-
-        x_train_words = x_train[:].bitcast(F32)
-        xt_codes, xt_scales = transpose_words_and_quantise(
-            nc, pools, ident, lambda t, u: x_train_words[:, t, u * P : (u + 1) * P], "x_train"
-        )
+        for g in range(1, AHEAD + 1):
+            chunks[g] = load_chunk(g)
 
         def spread_half_sx():
             squares_x = const.tile([P, TILES, DM], BF16, name="squares_x")
@@ -116,7 +125,7 @@ def tile_condtransportkernel_pa_t_kernel(
                     accum_out=sx[:, t : t + 1],
                 )
             repeated = const.tile([P, TILES, P], F32, name="repeated")
-            nc.vector.tensor_copy(
+            nc.gpsimd.tensor_copy(
                 out=repeated[:], in_=sx[:].unsqueeze(2).to_broadcast([P, TILES, P])
             )
             spread = pools["cross"].tile([P, NX], F32, name="cross")
@@ -125,21 +134,21 @@ def tile_condtransportkernel_pa_t_kernel(
                     out=spread[:, t * P : (t + 1) * P], in_=repeated[:, t, :], identity=ident[:]
                 )
             half_sx = const.tile([P, NX], F32, name="half_sx")
-            nc.scalar.mul(out=half_sx[:], in_=spread[:], mul=0.5)
+            nc.vector.tensor_scalar(
+                out=half_sx[:], in0=spread[:], scalar1=0.5, scalar2=None, op0=ALU.mult
+            )
             return half_sx
 
         def make_lam():
-            k_inv_words = k_inv[:].bitcast(F32)
-            ki_codes, ki_scales = transpose_words_and_quantise(
-                nc, pools, ident, lambda t, u: k_inv_words[:, t, u * P : (u + 1) * P], "k_inv"
-            )
             z_grouped = const.tile([P, DY, PACK], BF16, align_bytes=64, name="z_grouped")
             nc.vector.tensor_copy(out=z_grouped[:], in_=z_rows[:].rearrange("p t d -> p d t"))
-            z_codes, z_scales = mx_tiles(const, DY, "z")
-            nc.vector.quantize_mx(
-                out=z_codes[:].bitcast(FP8X4), scales=z_scales[:],
-                in_=z_grouped[:].rearrange("p d t -> p (d t)"),
+            k_inv_words = k_inv[:].bitcast(F32)
+            banks = transpose_words(
+                nc, pools, "flipped", ident, lambda t, u: k_inv_words[:, t, u * P : (u + 1) * P]
             )
+            ki_grouped = pair_words(nc.vector.tensor_copy, pools, banks)
+            z_codes, z_scales = quantise(nc, const, z_grouped, "z")
+            ki_codes, ki_scales = quantise(nc, const, ki_grouped, "k_inv")
             lam_grouped = const.tile([P, DY, PACK], BF16, align_bytes=64, name="lam_grouped")
             for b in range(2):
                 lam_psum = pools["product"].tile([P, 2, DY], F32, name="product")
@@ -156,21 +165,22 @@ def tile_condtransportkernel_pa_t_kernel(
                     out=lam_grouped[:, :, 2 * b : 2 * b + 2],
                     in_=lam_psum[:].rearrange("p t d -> p d t"),
                 )
-            lam_codes, lam_scales = mx_tiles(const, DY, "lam")
-            nc.vector.quantize_mx(
-                out=lam_codes[:].bitcast(FP8X4), scales=lam_scales[:],
-                in_=lam_grouped[:].rearrange("p d t -> p (d t)"),
-            )
-            return lam_codes, lam_scales
+            return quantise(nc, const, lam_grouped, "lam")
 
-        half_sx = spread_half_sx()
-        lam_codes, lam_scales = make_lam()
-
-        def prepare(c):
-            y_f32 = work.tile([P, TILES, DY], F32, name="y_f32")
-            nc.vector.tensor_tensor(out=y_f32[:], in0=c["ym"][:], in1=c["yv"][:], op=ALU.add)
+        def add_y(c):
             y_bf16 = work.tile([P, TILES, DY], BF16, name="y_bf16")
             nc.vector.tensor_tensor(out=y_bf16[:], in0=c["ym"][:], in1=c["yv"][:], op=ALU.add)
+            y_f32 = work.tile([P, TILES, DY], F32, name="y_f32")
+            nc.vector.tensor_tensor(out=y_f32[:], in0=c["ym"][:], in1=c["yv"][:], op=ALU.add)
+            xm_words = c["xm"][:].bitcast(F32)
+            y_words = y_bf16[:].bitcast(F32)
+            c["banks"] = transpose_words(
+                nc, pools, "planes", ident, lambda a, u: (xm_words, y_words)[u][:, a, :]
+            )
+            c["y_f32"] = y_f32
+
+        def pair_and_square(c):
+            c["grouped"] = pair_words(nc.scalar.copy, pools, c["banks"])
             squares = work.tile([P, 2 * TILES, DY], BF16, name="squares")
             sum_x = work.tile([P, TILES], F32, name="sum_x")
             sum_y = work.tile([P, TILES], F32, name="sum_y")
@@ -180,7 +190,7 @@ def tile_condtransportkernel_pa_t_kernel(
                     accum_out=sum_x[:, a : a + 1],
                 )
                 nc.scalar.activation(
-                    out=squares[:, 2 * a + 1, :], in_=y_f32[:, a, :], func=ACT.Square,
+                    out=squares[:, 2 * a + 1, :], in_=c["y_f32"][:, a, :], func=ACT.Square,
                     accum_out=sum_y[:, a : a + 1],
                 )
             sq = work.tile([P, TILES], F32, name="sq")
@@ -189,19 +199,15 @@ def tile_condtransportkernel_pa_t_kernel(
             nc.gpsimd.tensor_scalar(
                 out=half_sq[:], in0=sq[:], scalar1=0.5, scalar2=0.0, op0=ALU.mult, op1=ALU.add
             )
-            c["y_bf16"], c["half_sq"] = y_bf16, half_sq
+            c["half_sq"] = half_sq
 
         def quantise_queries(c):
-            xm_words = c["xm"][:].bitcast(F32)
-            y_words = c["y_bf16"][:].bitcast(F32)
-            c["query"] = transpose_words_and_quantise(
-                nc, pools, ident, lambda a, u: (xm_words, y_words)[u][:, a, :], "query"
-            )
+            c["query"] = quantise(nc, work, c["grouped"], "query")
+            c["minus_half_d2"] = work.tile([P, TILES, NX], F32, name="minus_half_d2")
 
-        def distances(c):
+        def distances(c, row_tiles):
             q_codes, q_scales = c["query"]
-            minus_half_d2 = work.tile([P, TILES, NX], F32, name="minus_half_d2")
-            for a in range(TILES):
+            for a in row_tiles:
                 cross = pools["cross"].tile([P, NX], F32, name="cross")
                 nc.tensor.matmul_mx(
                     out=cross[:],
@@ -212,12 +218,12 @@ def tile_condtransportkernel_pa_t_kernel(
                     start=True, stop=True,
                 )
                 nc.vector.scalar_tensor_tensor(
-                    out=minus_half_d2[:, a, :], in0=cross[:], scalar=c["half_sq"][:, a : a + 1],
-                    in1=half_sx[:], op0=ALU.subtract, op1=ALU.subtract,
+                    out=c["minus_half_d2"][:, a, :], in0=cross[:],
+                    scalar=c["half_sq"][:, a : a + 1], in1=half_sx[:],
+                    op0=ALU.subtract, op1=ALU.subtract,
                 )
-            c["minus_half_d2"] = minus_half_d2
 
-        def quantise_kernel(c):
+        def flip_and_exp(c):
             k_grouped = work.tile([P, CHUNK, PACK], BF16, align_bytes=64, name="k_grouped")
             for a in range(TILES):
                 flipped = pools["flipped"].tile([P, PACK, P], F32, name="flipped")
@@ -232,15 +238,18 @@ def tile_condtransportkernel_pa_t_kernel(
                     in_=flipped[:].rearrange("p t r -> p r t"),
                     func=ACT.Exp, scale=1.0 / 64.0,
                 )
-            flat = k_grouped[:].rearrange("p n t -> p (n t)")
-            nc.vector.tensor_scalar(out=flat, in0=flat, scalar1=1.0, scalar2=None, op0=ALU.min)
-            k_codes, k_scales = mx_tiles(work, CHUNK, "kernel")
-            nc.vector.quantize_mx(out=k_codes[:].bitcast(FP8X4), scales=k_scales[:], in_=flat)
-            c["kernel"] = (k_codes, k_scales)
+            c["k_grouped"] = k_grouped
 
-        def finish(g, c):
+        def clamp(c):
+            flat = c["k_grouped"][:].rearrange("p n t -> p (n t)")
+            nc.vector.tensor_scalar(out=flat, in0=flat, scalar1=1.0, scalar2=None, op0=ALU.min)
+
+        def quantise_kernel(c):
+            c["kernel"] = quantise(nc, work, c["k_grouped"], "kernel")
+
+        def products(c):
             k_codes, k_scales = c["kernel"]
-            result = work.tile([P, TILES, DY], F32, name="result")
+            c["products"] = []
             for b in range(TILES // 2):
                 product = pools["product"].tile([P, 2, DY], F32, name="product")
                 for a in (2 * b, 2 * b + 1):
@@ -252,6 +261,11 @@ def tile_condtransportkernel_pa_t_kernel(
                         rhs_scale=lam_scales[:],
                         start=True, stop=True,
                     )
+                c["products"].append(product)
+
+        def add_y_mean_and_store(g, c):
+            result = work.tile([P, TILES, DY], F32, name="result")
+            for b, product in enumerate(c["products"]):
                 nc.vector.tensor_tensor(
                     out=result[:, 2 * b : 2 * b + 2, :], in0=product[:],
                     in1=c["ym"][:, 2 * b : 2 * b + 2, :], op=ALU.add,
@@ -261,16 +275,39 @@ def tile_condtransportkernel_pa_t_kernel(
                 in_=result[:],
             )
 
-        for step in range(N_CHUNKS + STAGES - 1):
-            if step + 1 < N_CHUNKS:
-                chunks[step + 1] = load_chunk(step + 1)
-            if 0 <= step - 4:
-                finish(step - 4, chunks[step - 4])
-            if 0 <= step - 3 < N_CHUNKS:
+        x_train_words = x_train[:].bitcast(F32)
+        banks = transpose_words(
+            nc, pools, "planes", ident, lambda t, u: x_train_words[:, t, u * P : (u + 1) * P]
+        )
+        xt_codes, xt_scales = quantise(
+            nc, const, pair_words(nc.scalar.copy, pools, banks), "x_train"
+        )
+        add_y(chunks[0])
+        half_sx = spread_half_sx()
+        lam_codes, lam_scales = make_lam()
+
+        def live(g):
+            return 0 <= g < N_CHUNKS
+
+        for step in range(1, N_CHUNKS + OLDEST):
+            if live(step + AHEAD):
+                chunks[step + AHEAD] = load_chunk(step + AHEAD)
+            if live(step - 3):
+                clamp(chunks[step - 3])
+            if live(step - 4):
+                add_y_mean_and_store(step - 4, chunks[step - 4])
+            if live(step - 3):
                 quantise_kernel(chunks[step - 3])
-            if 0 <= step - 2 < N_CHUNKS:
-                distances(chunks[step - 2])
-            if 0 <= step - 1 < N_CHUNKS:
+            if live(step - 1):
+                pair_and_square(chunks[step - 1])
+            if live(step - 2):
+                distances(chunks[step - 2], (0, 1))
+            if live(step - 3):
+                products(chunks[step - 3])
+            if live(step - 2):
+                distances(chunks[step - 2], (2, 3))
+                flip_and_exp(chunks[step - 2])
+            if live(step - 1):
                 quantise_queries(chunks[step - 1])
-            if step < N_CHUNKS:
-                prepare(chunks[step])
+            if live(step):
+                add_y(chunks[step])

@@ -24,6 +24,7 @@ N_CHUNKS = NTEST // CHUNK
 HALF = 2 * P
 OLDEST = 4
 AHEAD = 2
+FILLING = 2
 
 FLOPS = 2 * (NX * NX * DY + NX * DM * NTEST + NTEST * NX * DY)
 
@@ -44,10 +45,10 @@ def quantise(nc, pool, grouped, name):
     return codes, scales
 
 
-def transpose_words(nc, pools, kind, ident, word_block):
+def transpose_words(nc, pools, ident, word_block):
     banks = []
     for b in range(CHUNK // HALF):
-        planes = pools[kind].tile([P, 2, HALF], F32, name=kind)
+        planes = pools["psum"].tile([P, 2, HALF], F32, name="bank")
         for a in range(HALF // P):
             for u in range(2):
                 nc.tensor.transpose(
@@ -80,12 +81,9 @@ def tile_condtransportkernel_pa_t_kernel(
         work = stack.enter_context(tc.tile_pool(name="work", bufs=3))
         pools = {
             "work": work,
-            "loads": stack.enter_context(tc.tile_pool(name="loads", bufs=AHEAD + 3)),
+            "loads": stack.enter_context(tc.tile_pool(name="loads", bufs=AHEAD + 4)),
             "y_mean": stack.enter_context(tc.tile_pool(name="y_mean", bufs=AHEAD + OLDEST + 2)),
-            "planes": stack.enter_context(tc.psum_pool(name="planes", bufs=2)),
-            "cross": stack.enter_context(tc.psum_pool(name="cross", bufs=2)),
-            "flipped": stack.enter_context(tc.psum_pool(name="flipped", bufs=2)),
-            "product": stack.enter_context(tc.psum_pool(name="product", bufs=2)),
+            "psum": stack.enter_context(tc.psum_pool(name="psum", bufs=8)),
         }
 
         ident = const.tile([P, P], F32, name="ident")
@@ -113,10 +111,10 @@ def tile_condtransportkernel_pa_t_kernel(
                 out=z_rows[:, 2 * u : 2 * u + 2, :],
                 in_=Z_mean[u * HALF : (u + 1) * HALF, :].rearrange("(q e) d -> q e d", e=2),
             )
-        for g in range(1, AHEAD + 1):
+        for g in range(1, AHEAD):
             chunks[g] = load_chunk(g)
 
-        def spread_half_sx():
+        def sum_squares_x():
             squares_x = const.tile([P, TILES, DM], BF16, name="squares_x")
             sx = const.tile([P, TILES], F32, name="sx")
             for t in range(TILES):
@@ -128,15 +126,16 @@ def tile_condtransportkernel_pa_t_kernel(
             nc.gpsimd.tensor_copy(
                 out=repeated[:], in_=sx[:].unsqueeze(2).to_broadcast([P, TILES, P])
             )
-            spread = pools["cross"].tile([P, NX], F32, name="cross")
+            return repeated
+
+        def spread_half_sx(repeated):
+            spread = pools["psum"].tile([P, NX], F32, name="bank")
             for t in range(TILES):
                 nc.tensor.transpose(
                     out=spread[:, t * P : (t + 1) * P], in_=repeated[:, t, :], identity=ident[:]
                 )
             half_sx = const.tile([P, NX], F32, name="half_sx")
-            nc.vector.tensor_scalar(
-                out=half_sx[:], in0=spread[:], scalar1=0.5, scalar2=None, op0=ALU.mult
-            )
+            nc.scalar.mul(out=half_sx[:], in_=spread[:], mul=0.5)
             return half_sx
 
         def make_lam():
@@ -144,14 +143,14 @@ def tile_condtransportkernel_pa_t_kernel(
             nc.vector.tensor_copy(out=z_grouped[:], in_=z_rows[:].rearrange("p t d -> p d t"))
             k_inv_words = k_inv[:].bitcast(F32)
             banks = transpose_words(
-                nc, pools, "flipped", ident, lambda t, u: k_inv_words[:, t, u * P : (u + 1) * P]
+                nc, pools, ident, lambda t, u: k_inv_words[:, t, u * P : (u + 1) * P]
             )
             ki_grouped = pair_words(nc.vector.tensor_copy, pools, banks)
             z_codes, z_scales = quantise(nc, const, z_grouped, "z")
             ki_codes, ki_scales = quantise(nc, const, ki_grouped, "k_inv")
             lam_grouped = const.tile([P, DY, PACK], BF16, align_bytes=64, name="lam_grouped")
             for b in range(2):
-                lam_psum = pools["product"].tile([P, 2, DY], F32, name="product")
+                lam_psum = pools["psum"].tile([P, 2, DY], F32, name="bank")
                 for t in (2 * b, 2 * b + 1):
                     nc.tensor.matmul_mx(
                         out=lam_psum[:, t - 2 * b, :],
@@ -167,34 +166,39 @@ def tile_condtransportkernel_pa_t_kernel(
                 )
             return quantise(nc, const, lam_grouped, "lam")
 
-        def add_y(c):
-            y_bf16 = work.tile([P, TILES, DY], BF16, name="y_bf16")
-            nc.vector.tensor_tensor(out=y_bf16[:], in0=c["ym"][:], in1=c["yv"][:], op=ALU.add)
-            y_f32 = work.tile([P, TILES, DY], F32, name="y_f32")
-            nc.vector.tensor_tensor(out=y_f32[:], in0=c["ym"][:], in1=c["yv"][:], op=ALU.add)
-            xm_words = c["xm"][:].bitcast(F32)
-            y_words = y_bf16[:].bitcast(F32)
-            c["banks"] = transpose_words(
-                nc, pools, "planes", ident, lambda a, u: (xm_words, y_words)[u][:, a, :]
+        def round_y(c):
+            c["y_bf16"] = work.tile([P, TILES, DY], BF16, name="y_bf16")
+            nc.vector.tensor_tensor(
+                out=c["y_bf16"][:], in0=c["ym"][:], in1=c["yv"][:], op=ALU.add
             )
-            c["y_f32"] = y_f32
 
-        def pair_and_square(c):
+        def transpose_queries(c):
+            xm_words = c["xm"][:].bitcast(F32)
+            y_words = c["y_bf16"][:].bitcast(F32)
+            c["banks"] = transpose_words(
+                nc, pools, ident, lambda a, u: (xm_words, y_words)[u][:, a, :]
+            )
+
+        def pair_queries(c):
             c["grouped"] = pair_words(nc.scalar.copy, pools, c["banks"])
-            squares = work.tile([P, 2 * TILES, DY], BF16, name="squares")
-            sum_x = work.tile([P, TILES], F32, name="sum_x")
-            sum_y = work.tile([P, TILES], F32, name="sum_y")
-            for a in range(TILES):
-                nc.scalar.activation(
-                    out=squares[:, 2 * a, :], in_=c["xm"][:, a, :], func=ACT.Square,
-                    accum_out=sum_x[:, a : a + 1],
-                )
-                nc.scalar.activation(
-                    out=squares[:, 2 * a + 1, :], in_=c["y_f32"][:, a, :], func=ACT.Square,
-                    accum_out=sum_y[:, a : a + 1],
-                )
+
+        def keep_y(c):
+            c["y_f32"] = work.tile([P, TILES, DY], F32, name="y_f32")
+            nc.vector.tensor_tensor(
+                out=c["y_f32"][:], in0=c["ym"][:], in1=c["yv"][:], op=ALU.add
+            )
+
+        def sum_squares(c):
+            squares = work.tile([P, 2, TILES, DY], BF16, name="squares")
+            sums = [work.tile([P, TILES], F32, name=name) for name in ("sum_x", "sum_y")]
+            for half, source in enumerate((c["xm"], c["y_f32"])):
+                for a in range(TILES):
+                    nc.scalar.activation(
+                        out=squares[:, half, a, :], in_=source[:, a, :], func=ACT.Square,
+                        accum_out=sums[half][:, a : a + 1],
+                    )
             sq = work.tile([P, TILES], F32, name="sq")
-            nc.gpsimd.tensor_tensor(out=sq[:], in0=sum_x[:], in1=sum_y[:], op=ALU.add)
+            nc.gpsimd.tensor_tensor(out=sq[:], in0=sums[0][:], in1=sums[1][:], op=ALU.add)
             half_sq = work.tile([P, TILES], F32, name="half_sq")
             nc.gpsimd.tensor_scalar(
                 out=half_sq[:], in0=sq[:], scalar1=0.5, scalar2=0.0, op0=ALU.mult, op1=ALU.add
@@ -205,10 +209,12 @@ def tile_condtransportkernel_pa_t_kernel(
             c["query"] = quantise(nc, work, c["grouped"], "query")
             c["minus_half_d2"] = work.tile([P, TILES, NX], F32, name="minus_half_d2")
 
-        def distances(c, row_tiles):
+        def cross_products(c):
             q_codes, q_scales = c["query"]
-            for a in row_tiles:
-                cross = pools["cross"].tile([P, NX], F32, name="cross")
+            xt_codes, xt_scales = train["x"]
+            c["cross"] = []
+            for a in range(TILES):
+                cross = pools["psum"].tile([P, NX], F32, name="bank")
                 nc.tensor.matmul_mx(
                     out=cross[:],
                     lhsT=q_codes[:, a * P : (a + 1) * P].bitcast(FP8X4),
@@ -217,16 +223,20 @@ def tile_condtransportkernel_pa_t_kernel(
                     rhs_scale=xt_scales[:],
                     start=True, stop=True,
                 )
+                c["cross"].append(cross)
+
+        def distances(c, row_tiles):
+            for a in row_tiles:
                 nc.vector.scalar_tensor_tensor(
-                    out=c["minus_half_d2"][:, a, :], in0=cross[:],
-                    scalar=c["half_sq"][:, a : a + 1], in1=half_sx[:],
+                    out=c["minus_half_d2"][:, a, :], in0=c["cross"][a][:],
+                    scalar=c["half_sq"][:, a : a + 1], in1=train["half_sx"][:],
                     op0=ALU.subtract, op1=ALU.subtract,
                 )
 
         def flip_and_exp(c):
             k_grouped = work.tile([P, CHUNK, PACK], BF16, align_bytes=64, name="k_grouped")
             for a in range(TILES):
-                flipped = pools["flipped"].tile([P, PACK, P], F32, name="flipped")
+                flipped = pools["psum"].tile([P, PACK, P], F32, name="bank")
                 for t in range(PACK):
                     nc.tensor.transpose(
                         out=flipped[:, t, :],
@@ -249,9 +259,10 @@ def tile_condtransportkernel_pa_t_kernel(
 
         def products(c):
             k_codes, k_scales = c["kernel"]
+            lam_codes, lam_scales = train["lam"]
             c["products"] = []
             for b in range(TILES // 2):
-                product = pools["product"].tile([P, 2, DY], F32, name="product")
+                product = pools["psum"].tile([P, 2, DY], F32, name="bank")
                 for a in (2 * b, 2 * b + 1):
                     nc.tensor.matmul_mx(
                         out=product[:, a - 2 * b, :],
@@ -275,39 +286,46 @@ def tile_condtransportkernel_pa_t_kernel(
                 in_=result[:],
             )
 
+        repeated_sx = sum_squares_x()
         x_train_words = x_train[:].bitcast(F32)
         banks = transpose_words(
-            nc, pools, "planes", ident, lambda t, u: x_train_words[:, t, u * P : (u + 1) * P]
+            nc, pools, ident, lambda t, u: x_train_words[:, t, u * P : (u + 1) * P]
         )
-        xt_codes, xt_scales = quantise(
-            nc, const, pair_words(nc.scalar.copy, pools, banks), "x_train"
-        )
-        add_y(chunks[0])
-        half_sx = spread_half_sx()
-        lam_codes, lam_scales = make_lam()
+        xt_grouped = pair_words(nc.scalar.copy, pools, banks)
+        train = {}
 
         def live(g):
             return 0 <= g < N_CHUNKS
 
-        for step in range(1, N_CHUNKS + OLDEST):
+        for step in range(N_CHUNKS + OLDEST):
             if live(step + AHEAD):
                 chunks[step + AHEAD] = load_chunk(step + AHEAD)
+            if live(step):
+                round_y(chunks[step])
+            if live(step - 2):
+                pair_queries(chunks[step - 2])
+                sum_squares(chunks[step - 2])
             if live(step - 3):
-                clamp(chunks[step - 3])
+                cross_products(chunks[step - 3])
+            if live(step - 4):
+                clamp(chunks[step - 4])
+            if live(step - 3):
+                distances(chunks[step - 3], (0,))
+            if live(step - 4):
+                quantise_kernel(chunks[step - 4])
+                products(chunks[step - 4])
+            if live(step - 3):
+                distances(chunks[step - 3], (1, 2, 3))
+                flip_and_exp(chunks[step - 3])
+            if live(step - 1):
+                transpose_queries(chunks[step - 1])
             if live(step - 4):
                 add_y_mean_and_store(step - 4, chunks[step - 4])
-            if live(step - 3):
-                quantise_kernel(chunks[step - 3])
-            if live(step - 1):
-                pair_and_square(chunks[step - 1])
             if live(step - 2):
-                distances(chunks[step - 2], (0, 1))
-            if live(step - 3):
-                products(chunks[step - 3])
-            if live(step - 2):
-                distances(chunks[step - 2], (2, 3))
-                flip_and_exp(chunks[step - 2])
-            if live(step - 1):
-                quantise_queries(chunks[step - 1])
+                quantise_queries(chunks[step - 2])
             if live(step):
-                add_y(chunks[step])
+                keep_y(chunks[step])
+            if step == FILLING:
+                train["x"] = quantise(nc, const, xt_grouped, "x_train")
+                train["lam"] = make_lam()
+                train["half_sx"] = spread_half_sx(repeated_sx)

@@ -60,15 +60,12 @@ def transpose_words(nc, pools, ident, word_block):
     return banks
 
 
-def pair_words(copy, pools, banks):
-    grouped = pools["work"].tile([P, CHUNK, PACK], BF16, align_bytes=64, name="grouped")
+def pair_words(copy, grouped, b, planes):
     grouped_words = grouped[:].bitcast(F32)
-    for b, planes in enumerate(banks):
-        copy(
-            out=grouped_words[:, b * HALF : (b + 1) * HALF, :],
-            in_=planes[:].rearrange("p u n -> p n u"),
-        )
-    return grouped
+    copy(
+        out=grouped_words[:, b * HALF : (b + 1) * HALF, :],
+        in_=planes[:].rearrange("p u n -> p n u"),
+    )
 
 
 def tile_condtransportkernel_pa_t_kernel(
@@ -83,6 +80,7 @@ def tile_condtransportkernel_pa_t_kernel(
             "work": work,
             "loads": stack.enter_context(tc.tile_pool(name="loads", bufs=AHEAD + 4)),
             "y_mean": stack.enter_context(tc.tile_pool(name="y_mean", bufs=AHEAD + OLDEST + 2)),
+            "y_f32": stack.enter_context(tc.tile_pool(name="y_f32", bufs=2)),
             "psum": stack.enter_context(tc.psum_pool(name="psum", bufs=8)),
         }
 
@@ -94,15 +92,17 @@ def tile_condtransportkernel_pa_t_kernel(
             xm = pools["loads"].tile([P, TILES, DX], BF16, name="xm")
             ym = pools["y_mean"].tile([P, TILES, DY], BF16, name="ym")
             yv = pools["loads"].tile([P, TILES, DY], BF16, name="yv")
-            for tile_, source in ((xm, x_mu), (ym, y_mean), (yv, y_var)):
+            for tile_, source in ((ym, y_mean), (yv, y_var), (xm, x_mu)):
                 nc.sync.dma_start(
                     out=tile_[:], in_=source[rows, :].rearrange("(p a) c -> p a c", a=TILES)
                 )
             return {"xm": xm, "ym": ym, "yv": yv}
 
+        chunks = {0: load_chunk(0)}
         x_train = const.tile([P, TILES, DM], BF16, name="x_train")
         nc.sync.dma_start(out=x_train[:], in_=X_mean.rearrange("(t p) c -> p t c", p=P))
-        chunks = {0: load_chunk(0)}
+        for g in range(1, AHEAD):
+            chunks[g] = load_chunk(g)
         k_inv = const.tile([P, TILES, NX], BF16, name="k_inv")
         nc.sync.dma_start(out=k_inv[:], in_=kXXmean_inv.rearrange("(t p) c -> p t c", p=P))
         z_rows = const.tile([P, PACK, DY], BF16, name="z_rows")
@@ -111,10 +111,8 @@ def tile_condtransportkernel_pa_t_kernel(
                 out=z_rows[:, 2 * u : 2 * u + 2, :],
                 in_=Z_mean[u * HALF : (u + 1) * HALF, :].rearrange("(q e) d -> q e d", e=2),
             )
-        for g in range(1, AHEAD):
-            chunks[g] = load_chunk(g)
 
-        def sum_squares_x():
+        def repeat_sx():
             squares_x = const.tile([P, TILES, DM], BF16, name="squares_x")
             sx = const.tile([P, TILES], F32, name="sx")
             for t in range(TILES):
@@ -145,7 +143,9 @@ def tile_condtransportkernel_pa_t_kernel(
             banks = transpose_words(
                 nc, pools, ident, lambda t, u: k_inv_words[:, t, u * P : (u + 1) * P]
             )
-            ki_grouped = pair_words(nc.vector.tensor_copy, pools, banks)
+            ki_grouped = work.tile([P, CHUNK, PACK], BF16, align_bytes=64, name="grouped")
+            for b, planes in enumerate(banks):
+                pair_words(nc.vector.tensor_copy, ki_grouped, b, planes)
             z_codes, z_scales = quantise(nc, const, z_grouped, "z")
             ki_codes, ki_scales = quantise(nc, const, ki_grouped, "k_inv")
             lam_grouped = const.tile([P, DY, PACK], BF16, align_bytes=64, name="lam_grouped")
@@ -179,31 +179,31 @@ def tile_condtransportkernel_pa_t_kernel(
                 nc, pools, ident, lambda a, u: (xm_words, y_words)[u][:, a, :]
             )
 
-        def pair_queries(c):
-            c["grouped"] = pair_words(nc.scalar.copy, pools, c["banks"])
-
         def keep_y(c):
-            c["y_f32"] = work.tile([P, TILES, DY], F32, name="y_f32")
-            nc.vector.tensor_tensor(
-                out=c["y_f32"][:], in0=c["ym"][:], in1=c["yv"][:], op=ALU.add
-            )
+            c["y_f32"] = pools["y_f32"].tile([P, TILES, DY], F32, name="y_f32")
+            for a in range(TILES):
+                nc.gpsimd.tensor_tensor(
+                    out=c["y_f32"][:, a, :], in0=c["ym"][:, a, :], in1=c["yv"][:, a, :],
+                    op=ALU.add,
+                )
 
-        def sum_squares(c):
-            squares = work.tile([P, 2, TILES, DY], BF16, name="squares")
-            sums = [work.tile([P, TILES], F32, name=name) for name in ("sum_x", "sum_y")]
-            for half, source in enumerate((c["xm"], c["y_f32"])):
-                for a in range(TILES):
-                    nc.scalar.activation(
-                        out=squares[:, half, a, :], in_=source[:, a, :], func=ACT.Square,
-                        accum_out=sums[half][:, a : a + 1],
-                    )
+        def sum_squares(c, source, name):
+            squares = work.tile([P, TILES, DY], BF16, name="squares_" + name)
+            c[name] = work.tile([P, TILES], F32, name=name)
+            for a in range(TILES):
+                nc.scalar.activation(
+                    out=squares[:, a, :], in_=source[:, a, :], func=ACT.Square,
+                    accum_out=c[name][:, a : a + 1],
+                )
+
+        def halve_sq(c):
             sq = work.tile([P, TILES], F32, name="sq")
-            nc.gpsimd.tensor_tensor(out=sq[:], in0=sums[0][:], in1=sums[1][:], op=ALU.add)
-            half_sq = work.tile([P, TILES], F32, name="half_sq")
+            nc.gpsimd.tensor_tensor(out=sq[:], in0=c["sum_x"][:], in1=c["sum_y"][:], op=ALU.add)
+            c["half_sq"] = work.tile([P, TILES], F32, name="half_sq")
             nc.gpsimd.tensor_scalar(
-                out=half_sq[:], in0=sq[:], scalar1=0.5, scalar2=0.0, op0=ALU.mult, op1=ALU.add
+                out=c["half_sq"][:], in0=sq[:], scalar1=0.5, scalar2=0.0,
+                op0=ALU.mult, op1=ALU.add,
             )
-            c["half_sq"] = half_sq
 
         def quantise_queries(c):
             c["query"] = quantise(nc, work, c["grouped"], "query")
@@ -225,8 +225,8 @@ def tile_condtransportkernel_pa_t_kernel(
                 )
                 c["cross"].append(cross)
 
-        def distances(c, row_tiles):
-            for a in row_tiles:
+        def distances(c):
+            for a in range(TILES):
                 nc.vector.scalar_tensor_tensor(
                     out=c["minus_half_d2"][:, a, :], in0=c["cross"][a][:],
                     scalar=c["half_sq"][:, a : a + 1], in1=train["half_sx"][:],
@@ -275,23 +275,23 @@ def tile_condtransportkernel_pa_t_kernel(
                 c["products"].append(product)
 
         def add_y_mean_and_store(g, c):
+            rows = out[g * CHUNK : (g + 1) * CHUNK, :].rearrange("(p a) d -> p a d", a=TILES)
             result = work.tile([P, TILES, DY], F32, name="result")
             for b, product in enumerate(c["products"]):
+                pair = slice(2 * b, 2 * b + 2)
                 nc.vector.tensor_tensor(
-                    out=result[:, 2 * b : 2 * b + 2, :], in0=product[:],
-                    in1=c["ym"][:, 2 * b : 2 * b + 2, :], op=ALU.add,
+                    out=result[:, pair, :], in0=product[:], in1=c["ym"][:, pair, :], op=ALU.add
                 )
-            nc.sync.dma_start(
-                out=out[g * CHUNK : (g + 1) * CHUNK, :].rearrange("(p a) d -> p a d", a=TILES),
-                in_=result[:],
-            )
+                nc.sync.dma_start(out=rows[:, pair, :], in_=result[:, pair, :])
 
-        repeated_sx = sum_squares_x()
+        repeated_sx = repeat_sx()
         x_train_words = x_train[:].bitcast(F32)
         banks = transpose_words(
             nc, pools, ident, lambda t, u: x_train_words[:, t, u * P : (u + 1) * P]
         )
-        xt_grouped = pair_words(nc.scalar.copy, pools, banks)
+        xt_grouped = work.tile([P, CHUNK, PACK], BF16, align_bytes=64, name="grouped")
+        for b, planes in enumerate(banks):
+            pair_words(nc.scalar.copy, xt_grouped, b, planes)
         train = {}
 
         def live(g):
@@ -300,31 +300,37 @@ def tile_condtransportkernel_pa_t_kernel(
         for step in range(N_CHUNKS + OLDEST):
             if live(step + AHEAD):
                 chunks[step + AHEAD] = load_chunk(step + AHEAD)
-            if live(step):
-                round_y(chunks[step])
             if live(step - 2):
-                pair_queries(chunks[step - 2])
-                sum_squares(chunks[step - 2])
+                sum_squares(chunks[step - 2], chunks[step - 2]["y_f32"], "sum_y")
+            if live(step):
+                keep_y(chunks[step])
+            if live(step - 2):
+                c = chunks[step - 2]
+                c["grouped"] = work.tile([P, CHUNK, PACK], BF16, align_bytes=64, name="grouped")
+                pair_words(nc.scalar.copy, c["grouped"], 0, c["banks"][0])
+                sum_squares(c, c["xm"], "sum_x")
+                halve_sq(c)
             if live(step - 3):
                 cross_products(chunks[step - 3])
             if live(step - 4):
                 clamp(chunks[step - 4])
-            if live(step - 3):
-                distances(chunks[step - 3], (0,))
+            if live(step):
+                round_y(chunks[step])
             if live(step - 4):
                 quantise_kernel(chunks[step - 4])
                 products(chunks[step - 4])
             if live(step - 3):
-                distances(chunks[step - 3], (1, 2, 3))
+                distances(chunks[step - 3])
                 flip_and_exp(chunks[step - 3])
             if live(step - 1):
                 transpose_queries(chunks[step - 1])
+            if live(step - 2):
+                c = chunks[step - 2]
+                pair_words(nc.vector.tensor_copy, c["grouped"], 1, c["banks"][1])
             if live(step - 4):
                 add_y_mean_and_store(step - 4, chunks[step - 4])
             if live(step - 2):
                 quantise_queries(chunks[step - 2])
-            if live(step):
-                keep_y(chunks[step])
             if step == FILLING:
                 train["x"] = quantise(nc, const, xt_grouped, "x_train")
                 train["lam"] = make_lam()

@@ -22,9 +22,12 @@ CHUNK = 512
 TILES = CHUNK // P
 N_CHUNKS = NTEST // CHUNK
 HALF = 2 * P
-OLDEST = 4
 AHEAD = 2
-FILLING = 2
+AGE_PAIR = 1
+AGE_CROSS = 2
+AGE_EXP = 3
+AGE_KERNEL = 4
+AGE_OUT = 5
 
 FLOPS = 2 * (NX * NX * DY + NX * DM * NTEST + NTEST * NX * DY)
 
@@ -77,9 +80,8 @@ def tile_condtransportkernel_pa_t_kernel(
         const = stack.enter_context(tc.tile_pool(name="const", bufs=1))
         work = stack.enter_context(tc.tile_pool(name="work", bufs=3))
         pools = {
-            "work": work,
-            "loads": stack.enter_context(tc.tile_pool(name="loads", bufs=AHEAD + 4)),
-            "y_mean": stack.enter_context(tc.tile_pool(name="y_mean", bufs=AHEAD + OLDEST + 2)),
+            "loads": stack.enter_context(tc.tile_pool(name="loads", bufs=AHEAD + AGE_PAIR + 2)),
+            "y_mean": stack.enter_context(tc.tile_pool(name="y_mean", bufs=AHEAD + AGE_OUT + 2)),
             "y_f32": stack.enter_context(tc.tile_pool(name="y_f32", bufs=2)),
             "psum": stack.enter_context(tc.psum_pool(name="psum", bufs=8)),
         }
@@ -98,10 +100,10 @@ def tile_condtransportkernel_pa_t_kernel(
                 )
             return {"xm": xm, "ym": ym, "yv": yv}
 
-        chunks = {0: load_chunk(0)}
         x_train = const.tile([P, TILES, DM], BF16, name="x_train")
         nc.sync.dma_start(out=x_train[:], in_=X_mean.rearrange("(t p) c -> p t c", p=P))
-        for g in range(1, AHEAD):
+        chunks = {}
+        for g in range(AHEAD):
             chunks[g] = load_chunk(g)
         k_inv = const.tile([P, TILES, NX], BF16, name="k_inv")
         nc.sync.dma_start(out=k_inv[:], in_=kXXmean_inv.rearrange("(t p) c -> p t c", p=P))
@@ -112,31 +114,36 @@ def tile_condtransportkernel_pa_t_kernel(
                 in_=Z_mean[u * HALF : (u + 1) * HALF, :].rearrange("(q e) d -> q e d", e=2),
             )
 
-        def repeat_sx():
+        train = {}
+
+        def square_and_transpose_x_train():
             squares_x = const.tile([P, TILES, DM], BF16, name="squares_x")
-            sx = const.tile([P, TILES], F32, name="sx")
+            train["sx"] = const.tile([P, TILES], F32, name="sx")
             for t in range(TILES):
                 nc.scalar.activation(
                     out=squares_x[:, t, :], in_=x_train[:, t, :], func=ACT.Square,
-                    accum_out=sx[:, t : t + 1],
+                    accum_out=train["sx"][:, t : t + 1],
                 )
-            repeated = const.tile([P, TILES, P], F32, name="repeated")
-            nc.gpsimd.tensor_copy(
-                out=repeated[:], in_=sx[:].unsqueeze(2).to_broadcast([P, TILES, P])
+            x_train_words = x_train[:].bitcast(F32)
+            banks = transpose_words(
+                nc, pools, ident, lambda t, u: x_train_words[:, t, u * P : (u + 1) * P]
             )
-            return repeated
+            train["xt_grouped"] = work.tile([P, CHUNK, PACK], BF16, align_bytes=64, name="grouped")
+            for b, planes in enumerate(banks):
+                pair_words(nc.scalar.copy, train["xt_grouped"], b, planes)
 
-        def spread_half_sx(repeated):
+        def spread_half_sx():
             spread = pools["psum"].tile([P, NX], F32, name="bank")
             for t in range(TILES):
                 nc.tensor.transpose(
-                    out=spread[:, t * P : (t + 1) * P], in_=repeated[:, t, :], identity=ident[:]
+                    out=spread[:, t * P : (t + 1) * P],
+                    in_=train["sx"][:, t : t + 1].to_broadcast([P, P]),
+                    identity=ident[:],
                 )
-            half_sx = const.tile([P, NX], F32, name="half_sx")
-            nc.scalar.mul(out=half_sx[:], in_=spread[:], mul=0.5)
-            return half_sx
+            train["half_sx"] = const.tile([P, NX], F32, name="half_sx")
+            nc.scalar.mul(out=train["half_sx"][:], in_=spread[:], mul=0.5)
 
-        def make_lam():
+        def quantise_lam_operands():
             z_grouped = const.tile([P, DY, PACK], BF16, align_bytes=64, name="z_grouped")
             nc.vector.tensor_copy(out=z_grouped[:], in_=z_rows[:].rearrange("p t d -> p d t"))
             k_inv_words = k_inv[:].bitcast(F32)
@@ -146,8 +153,12 @@ def tile_condtransportkernel_pa_t_kernel(
             ki_grouped = work.tile([P, CHUNK, PACK], BF16, align_bytes=64, name="grouped")
             for b, planes in enumerate(banks):
                 pair_words(nc.vector.tensor_copy, ki_grouped, b, planes)
-            z_codes, z_scales = quantise(nc, const, z_grouped, "z")
-            ki_codes, ki_scales = quantise(nc, const, ki_grouped, "k_inv")
+            train["z"] = quantise(nc, const, z_grouped, "z")
+            train["k_inv"] = quantise(nc, const, ki_grouped, "k_inv")
+
+        def make_lam():
+            ki_codes, ki_scales = train["k_inv"]
+            z_codes, z_scales = train["z"]
             lam_grouped = const.tile([P, DY, PACK], BF16, align_bytes=64, name="lam_grouped")
             for b in range(2):
                 lam_psum = pools["psum"].tile([P, 2, DY], F32, name="bank")
@@ -164,19 +175,12 @@ def tile_condtransportkernel_pa_t_kernel(
                     out=lam_grouped[:, :, 2 * b : 2 * b + 2],
                     in_=lam_psum[:].rearrange("p t d -> p d t"),
                 )
-            return quantise(nc, const, lam_grouped, "lam")
+            train["lam"] = quantise(nc, const, lam_grouped, "lam")
 
         def round_y(c):
             c["y_bf16"] = work.tile([P, TILES, DY], BF16, name="y_bf16")
             nc.vector.tensor_tensor(
                 out=c["y_bf16"][:], in0=c["ym"][:], in1=c["yv"][:], op=ALU.add
-            )
-
-        def transpose_queries(c):
-            xm_words = c["xm"][:].bitcast(F32)
-            y_words = c["y_bf16"][:].bitcast(F32)
-            c["banks"] = transpose_words(
-                nc, pools, ident, lambda a, u: (xm_words, y_words)[u][:, a, :]
             )
 
         def keep_y(c):
@@ -186,6 +190,18 @@ def tile_condtransportkernel_pa_t_kernel(
                     out=c["y_f32"][:, a, :], in0=c["ym"][:, a, :], in1=c["yv"][:, a, :],
                     op=ALU.add,
                 )
+
+        def transpose_queries(c):
+            xm_words = c["xm"][:].bitcast(F32)
+            y_words = c["y_bf16"][:].bitcast(F32)
+            c["banks"] = transpose_words(
+                nc, pools, ident, lambda a, u: (xm_words, y_words)[u][:, a, :]
+            )
+
+        def pair_queries(c):
+            c["grouped"] = work.tile([P, CHUNK, PACK], BF16, align_bytes=64, name="grouped")
+            pair_words(nc.scalar.copy, c["grouped"], 0, c["banks"][0])
+            pair_words(nc.vector.tensor_copy, c["grouped"], 1, c["banks"][1])
 
         def sum_squares(c, source, name):
             squares = work.tile([P, TILES, DY], BF16, name="squares_" + name)
@@ -207,7 +223,6 @@ def tile_condtransportkernel_pa_t_kernel(
 
         def quantise_queries(c):
             c["query"] = quantise(nc, work, c["grouped"], "query")
-            c["minus_half_d2"] = work.tile([P, TILES, NX], F32, name="minus_half_d2")
 
         def cross_products(c):
             q_codes, q_scales = c["query"]
@@ -226,6 +241,7 @@ def tile_condtransportkernel_pa_t_kernel(
                 c["cross"].append(cross)
 
         def distances(c):
+            c["minus_half_d2"] = work.tile([P, TILES, NX], F32, name="minus_half_d2")
             for a in range(TILES):
                 nc.vector.scalar_tensor_tensor(
                     out=c["minus_half_d2"][:, a, :], in0=c["cross"][a][:],
@@ -284,54 +300,43 @@ def tile_condtransportkernel_pa_t_kernel(
                 )
                 nc.sync.dma_start(out=rows[:, pair, :], in_=result[:, pair, :])
 
-        repeated_sx = repeat_sx()
-        x_train_words = x_train[:].bitcast(F32)
-        banks = transpose_words(
-            nc, pools, ident, lambda t, u: x_train_words[:, t, u * P : (u + 1) * P]
-        )
-        xt_grouped = work.tile([P, CHUNK, PACK], BF16, align_bytes=64, name="grouped")
-        for b, planes in enumerate(banks):
-            pair_words(nc.scalar.copy, xt_grouped, b, planes)
-        train = {}
+        def at_age(step, age):
+            return [g for g in (step - age,) if 0 <= g < N_CHUNKS]
 
-        def live(g):
-            return 0 <= g < N_CHUNKS
-
-        for step in range(N_CHUNKS + OLDEST):
-            if live(step + AHEAD):
-                chunks[step + AHEAD] = load_chunk(step + AHEAD)
-            if live(step - 2):
-                sum_squares(chunks[step - 2], chunks[step - 2]["y_f32"], "sum_y")
-            if live(step):
-                keep_y(chunks[step])
-            if live(step - 2):
-                c = chunks[step - 2]
-                c["grouped"] = work.tile([P, CHUNK, PACK], BF16, align_bytes=64, name="grouped")
-                pair_words(nc.scalar.copy, c["grouped"], 0, c["banks"][0])
-                sum_squares(c, c["xm"], "sum_x")
-                halve_sq(c)
-            if live(step - 3):
-                cross_products(chunks[step - 3])
-            if live(step - 4):
-                clamp(chunks[step - 4])
-            if live(step):
-                round_y(chunks[step])
-            if live(step - 4):
-                quantise_kernel(chunks[step - 4])
-                products(chunks[step - 4])
-            if live(step - 3):
-                distances(chunks[step - 3])
-                flip_and_exp(chunks[step - 3])
-            if live(step - 1):
-                transpose_queries(chunks[step - 1])
-            if live(step - 2):
-                c = chunks[step - 2]
-                pair_words(nc.vector.tensor_copy, c["grouped"], 1, c["banks"][1])
-            if live(step - 4):
-                add_y_mean_and_store(step - 4, chunks[step - 4])
-            if live(step - 2):
-                quantise_queries(chunks[step - 2])
-            if step == FILLING:
-                train["x"] = quantise(nc, const, xt_grouped, "x_train")
-                train["lam"] = make_lam()
-                train["half_sx"] = spread_half_sx(repeated_sx)
+        square_and_transpose_x_train()
+        for step in range(N_CHUNKS + AGE_OUT):
+            for g in at_age(step, -AHEAD):
+                chunks[g] = load_chunk(g)
+            for g in at_age(step, AGE_OUT):
+                products(chunks[g])
+            for g in at_age(step, AGE_CROSS):
+                cross_products(chunks[g])
+            for g in at_age(step, AGE_KERNEL):
+                clamp(chunks[g])
+            for g in at_age(step, 0):
+                round_y(chunks[g])
+            for g in at_age(step, AGE_KERNEL):
+                quantise_kernel(chunks[g])
+            for g in at_age(step, AGE_PAIR):
+                pair_queries(chunks[g])
+                sum_squares(chunks[g], chunks[g]["xm"], "sum_x")
+                sum_squares(chunks[g], chunks[g]["y_f32"], "sum_y")
+                halve_sq(chunks[g])
+            for g in at_age(step, 0):
+                keep_y(chunks[g])
+            for g in at_age(step, AGE_CROSS):
+                distances(chunks[g])
+            for g in at_age(step, AGE_EXP):
+                flip_and_exp(chunks[g])
+            for g in at_age(step, 0):
+                transpose_queries(chunks[g])
+            for g in at_age(step, AGE_OUT):
+                add_y_mean_and_store(g, chunks[g])
+            for g in at_age(step, AGE_PAIR):
+                quantise_queries(chunks[g])
+            if step == AGE_CROSS - 1:
+                train["x"] = quantise(nc, const, train["xt_grouped"], "x_train")
+                spread_half_sx()
+                quantise_lam_operands()
+            if step == AGE_CROSS:
+                make_lam()

@@ -82,12 +82,14 @@ def tile_condtransportkernel_pa_t_kernel(
         pools = {
             "loads": stack.enter_context(tc.tile_pool(name="loads", bufs=AHEAD + AGE_PAIR + 2)),
             "y_mean": stack.enter_context(tc.tile_pool(name="y_mean", bufs=AHEAD + AGE_OUT + 2)),
-            "y_f32": stack.enter_context(tc.tile_pool(name="y_f32", bufs=2)),
+            "y_f32": stack.enter_context(tc.tile_pool(name="y_f32", bufs=3)),
             "psum": stack.enter_context(tc.psum_pool(name="psum", bufs=8)),
         }
 
         ident = const.tile([P, P], F32, name="ident")
         make_identity(nc, ident[:])
+        ident_bf16 = const.tile([P, P], BF16, name="ident_bf16")
+        make_identity(nc, ident_bf16[:])
 
         def load_chunk(g):
             rows = slice(g * CHUNK, (g + 1) * CHUNK)
@@ -184,12 +186,17 @@ def tile_condtransportkernel_pa_t_kernel(
             )
 
         def keep_y(c):
-            c["y_f32"] = pools["y_f32"].tile([P, TILES, DY], F32, name="y_f32")
-            for a in range(TILES):
-                nc.gpsimd.tensor_tensor(
-                    out=c["y_f32"][:, a, :], in0=c["ym"][:, a, :], in1=c["yv"][:, a, :],
-                    op=ALU.add,
-                )
+            c["y_f32"] = pools["y_f32"].tile([P, 2, DY], F32, name="y_f32")
+            nc.vector.tensor_tensor(
+                out=c["y_f32"][:], in0=c["ym"][:, 0:2, :], in1=c["yv"][:, 0:2, :], op=ALU.add
+            )
+            c["y_psum"] = pools["psum"].tile([P, 2, DY], F32, name="bank")
+            for a in range(2):
+                for name in ("ym", "yv"):
+                    nc.tensor.matmul(
+                        c["y_psum"][:, a, :], lhsT=ident_bf16[:], rhs=c[name][:, 2 + a, :],
+                        start=name == "ym", stop=name == "yv",
+                    )
 
         def transpose_queries(c):
             xm_words = c["xm"][:].bitcast(F32)
@@ -203,12 +210,12 @@ def tile_condtransportkernel_pa_t_kernel(
             pair_words(nc.scalar.copy, c["grouped"], 0, c["banks"][0])
             pair_words(nc.vector.tensor_copy, c["grouped"], 1, c["banks"][1])
 
-        def sum_squares(c, source, name):
+        def sum_squares(c, sources, name):
             squares = work.tile([P, TILES, DY], BF16, name="squares_" + name)
             c[name] = work.tile([P, TILES], F32, name=name)
-            for a in range(TILES):
+            for a, source in sources:
                 nc.scalar.activation(
-                    out=squares[:, a, :], in_=source[:, a, :], func=ACT.Square,
+                    out=squares[:, a, :], in_=source, func=ACT.Square,
                     accum_out=c[name][:, a : a + 1],
                 )
 
@@ -319,16 +326,21 @@ def tile_condtransportkernel_pa_t_kernel(
                 quantise_kernel(chunks[g])
             for g in at_age(step, AGE_PAIR):
                 pair_queries(chunks[g])
-                sum_squares(chunks[g], chunks[g]["xm"], "sum_x")
-                sum_squares(chunks[g], chunks[g]["y_f32"], "sum_y")
-                halve_sq(chunks[g])
-            for g in at_age(step, 0):
-                keep_y(chunks[g])
+                c = chunks[g]
+                sum_squares(
+                    c,
+                    [(2 + a, c["y_psum"][:, a, :]) for a in range(2)]
+                    + [(a, c["y_f32"][:, a, :]) for a in range(2)],
+                    "sum_y",
+                )
+                sum_squares(c, [(a, c["xm"][:, a, :]) for a in range(TILES)], "sum_x")
+                halve_sq(c)
             for g in at_age(step, AGE_CROSS):
                 distances(chunks[g])
             for g in at_age(step, AGE_EXP):
                 flip_and_exp(chunks[g])
             for g in at_age(step, 0):
+                keep_y(chunks[g])
                 transpose_queries(chunks[g])
             for g in at_age(step, AGE_OUT):
                 add_y_mean_and_store(g, chunks[g])

@@ -144,6 +144,8 @@ def tile_condtransportkernel_pa_t_kernel(
                 )
             train["half_sx"] = const.tile([P, NX], F32, name="half_sx")
             nc.scalar.mul(out=train["half_sx"][:], in_=spread[:], mul=0.5)
+            train["minus_half_sx"] = const.tile([P, NX], F32, name="minus_half_sx")
+            nc.scalar.mul(out=train["minus_half_sx"][:], in_=spread[:], mul=-0.5)
 
         def quantise_lam_operands():
             z_grouped = const.tile([P, DY, PACK], BF16, align_bytes=64, name="z_grouped")
@@ -208,7 +210,7 @@ def tile_condtransportkernel_pa_t_kernel(
         def pair_queries(c):
             c["grouped"] = work.tile([P, CHUNK, PACK], BF16, align_bytes=64, name="grouped")
             pair_words(nc.scalar.copy, c["grouped"], 0, c["banks"][0])
-            pair_words(nc.vector.tensor_copy, c["grouped"], 1, c["banks"][1])
+            pair_words(nc.scalar.copy, c["grouped"], 1, c["banks"][1])
 
         def sum_squares(c, sources, name):
             squares = work.tile([P, TILES, DY], BF16, name="squares_" + name)
@@ -253,7 +255,7 @@ def tile_condtransportkernel_pa_t_kernel(
                 nc.vector.scalar_tensor_tensor(
                     out=c["minus_half_d2"][:, a, :], in0=c["cross"][a][:],
                     scalar=c["half_sq"][:, a : a + 1], in1=train["half_sx"][:],
-                    op0=ALU.subtract, op1=ALU.subtract,
+                    op0=ALU.subtract, op1=ALU.min,
                 )
 
         def flip_and_exp(c):
@@ -261,10 +263,14 @@ def tile_condtransportkernel_pa_t_kernel(
             for a in range(TILES):
                 flipped = pools["psum"].tile([P, PACK, P], F32, name="bank")
                 for t in range(PACK):
-                    nc.tensor.transpose(
-                        out=flipped[:, t, :],
-                        in_=c["minus_half_d2"][:, a, t * P : (t + 1) * P],
-                        identity=ident[:],
+                    cols = slice(t * P, (t + 1) * P)
+                    nc.tensor.matmul(
+                        flipped[:, t, :], lhsT=c["minus_half_d2"][:, a, cols], rhs=ident[:],
+                        is_transpose=True, start=True, stop=False,
+                    )
+                    nc.tensor.matmul(
+                        flipped[:, t, :], lhsT=train["minus_half_sx"][:, cols], rhs=ident[:],
+                        is_transpose=True, start=False, stop=True,
                     )
                 nc.scalar.activation(
                     out=k_grouped[:, a * P : (a + 1) * P, :],
@@ -272,10 +278,6 @@ def tile_condtransportkernel_pa_t_kernel(
                     func=ACT.Exp, scale=1.0 / 64.0,
                 )
             c["k_grouped"] = k_grouped
-
-        def clamp(c):
-            flat = c["k_grouped"][:].rearrange("p n t -> p (n t)")
-            nc.vector.tensor_scalar(out=flat, in0=flat, scalar1=1.0, scalar2=None, op0=ALU.min)
 
         def quantise_kernel(c):
             c["kernel"] = quantise(nc, work, c["k_grouped"], "kernel")
@@ -318,8 +320,6 @@ def tile_condtransportkernel_pa_t_kernel(
                 products(chunks[g])
             for g in at_age(step, AGE_CROSS):
                 cross_products(chunks[g])
-            for g in at_age(step, AGE_KERNEL):
-                clamp(chunks[g])
             for g in at_age(step, 0):
                 round_y(chunks[g])
             for g in at_age(step, AGE_KERNEL):

@@ -23,10 +23,15 @@ TILES = CHUNK // P
 N_CHUNKS = NTEST // CHUNK
 HALF = 2 * P
 AHEAD = 2
+AGE_Y = -1
+FIRST = 3
 AGE_PAIR = 1
 AGE_CROSS = 2
 AGE_EXP = 3
 AGE_KERNEL = 4
+T_CLAMP = 2
+S_EXTRA = 1
+LAST = 1
 AGE_OUT = 5
 
 FLOPS = 2 * (NX * NX * DY + NX * DM * NTEST + NTEST * NX * DY)
@@ -82,7 +87,7 @@ def tile_condtransportkernel_pa_t_kernel(
         pools = {
             "loads": stack.enter_context(tc.tile_pool(name="loads", bufs=AHEAD + AGE_PAIR + 2)),
             "y_mean": stack.enter_context(tc.tile_pool(name="y_mean", bufs=AHEAD + AGE_OUT + 2)),
-            "y_f32": stack.enter_context(tc.tile_pool(name="y_f32", bufs=3)),
+            "y_f32": stack.enter_context(tc.tile_pool(name="y_f32", bufs=4)),
             "psum": stack.enter_context(tc.psum_pool(name="psum", bufs=8)),
         }
 
@@ -131,8 +136,11 @@ def tile_condtransportkernel_pa_t_kernel(
                 nc, pools, ident, lambda t, u: x_train_words[:, t, u * P : (u + 1) * P]
             )
             train["xt_grouped"] = work.tile([P, CHUNK, PACK], BF16, align_bytes=64, name="grouped")
-            for b, planes in enumerate(banks):
-                pair_words(nc.scalar.copy, train["xt_grouped"], b, planes)
+            train["xt_banks"] = banks
+
+        def pair_x_train():
+            for b, planes in enumerate(train["xt_banks"]):
+                pair_words(nc.vector.tensor_copy, train["xt_grouped"], b, planes)
 
         def spread_half_sx():
             spread = pools["psum"].tile([P, NX], F32, name="bank")
@@ -181,24 +189,49 @@ def tile_condtransportkernel_pa_t_kernel(
                 )
             train["lam"] = quantise(nc, const, lam_grouped, "lam")
 
-        def round_y(c):
+        def round_y(g, c):
             c["y_bf16"] = work.tile([P, TILES, DY], BF16, name="y_bf16")
-            nc.vector.tensor_tensor(
-                out=c["y_bf16"][:], in0=c["ym"][:], in1=c["yv"][:], op=ALU.add
-            )
+            if g < FIRST:
+                nc.vector.tensor_tensor(
+                    out=c["y_bf16"][:], in0=c["ym"][:], in1=c["yv"][:], op=ALU.add
+                )
+            else:
+                c["y_f32"] = pools["y_f32"].tile([P, 2, DY], F32, name="y_f32")
+                nc.vector.memset(c["y_f32"][:, 0, 0:1], 0.0)
 
-        def keep_y(c):
-            c["y_f32"] = pools["y_f32"].tile([P, 2, DY], F32, name="y_f32")
-            nc.vector.tensor_tensor(
-                out=c["y_f32"][:], in0=c["ym"][:, 0:2, :], in1=c["yv"][:, 0:2, :], op=ALU.add
-            )
-            c["y_psum"] = pools["psum"].tile([P, 2, DY], F32, name="bank")
+        def make_y(g, c):
+            if g < FIRST:
+                return
             for a in range(2):
-                for name in ("ym", "yv"):
-                    nc.tensor.matmul(
-                        c["y_psum"][:, a, :], lhsT=ident_bf16[:], rhs=c[name][:, 2 + a, :],
-                        start=name == "ym", stop=name == "yv",
-                    )
+                nc.gpsimd.tensor_tensor(
+                    out=c["y_f32"][:, a, :], in0=c["ym"][:, a, :], in1=c["yv"][:, a, :],
+                    op=ALU.add,
+                )
+            for a in range(2, 4):
+                nc.gpsimd.tensor_tensor(
+                    out=c["y_bf16"][:, a, :], in0=c["ym"][:, a, :], in1=c["yv"][:, a, :],
+                    op=ALU.add,
+                )
+            for a in range(2):
+                nc.gpsimd.tensor_scalar(
+                    out=c["y_bf16"][:, a, :], in0=c["y_f32"][:, a, :], scalar1=1.0, scalar2=0.0,
+                    op0=ALU.mult, op1=ALU.add,
+                )
+
+        def keep_y(g, c):
+            c["y_rows"] = []
+            for b in ([0] if g < FIRST else []) + [1]:
+                y_psum = pools["psum"].tile([P, 2, DY], F32, name="bank")
+                for a in range(2):
+                    for name in ("ym", "yv"):
+                        nc.tensor.matmul(
+                            y_psum[:, a, :], lhsT=ident_bf16[:], rhs=c[name][:, 2 * b + a, :],
+                            start=name == "ym", stop=name == "yv",
+                        )
+                    c["y_rows"].append((2 * b + a, y_psum[:, a, :]))
+            if g >= FIRST:
+                for a in range(2):
+                    c["y_rows"].append((a, c["y_f32"][:, a, :]))
 
         def transpose_queries(c):
             xm_words = c["xm"][:].bitcast(F32)
@@ -207,10 +240,13 @@ def tile_condtransportkernel_pa_t_kernel(
                 nc, pools, ident, lambda a, u: (xm_words, y_words)[u][:, a, :]
             )
 
-        def pair_queries(c):
+        def pair_queries(g, c):
             c["grouped"] = work.tile([P, CHUNK, PACK], BF16, align_bytes=64, name="grouped")
             pair_words(nc.scalar.copy, c["grouped"], 0, c["banks"][0])
-            pair_words(nc.scalar.copy, c["grouped"], 1, c["banks"][1])
+            pair_words(
+                nc.scalar.copy if g < AGE_EXP - AGE_PAIR + S_EXTRA else nc.vector.tensor_copy,
+                c["grouped"], 1, c["banks"][1],
+            )
 
         def sum_squares(c, sources, name):
             squares = work.tile([P, TILES, DY], BF16, name="squares_" + name)
@@ -226,7 +262,7 @@ def tile_condtransportkernel_pa_t_kernel(
             nc.gpsimd.tensor_tensor(out=sq[:], in0=c["sum_x"][:], in1=c["sum_y"][:], op=ALU.add)
             c["half_sq"] = work.tile([P, TILES], F32, name="half_sq")
             nc.gpsimd.tensor_scalar(
-                out=c["half_sq"][:], in0=sq[:], scalar1=0.5, scalar2=0.0,
+                out=c["half_sq"][:], in0=sq[:], scalar1=-0.5, scalar2=0.0,
                 op0=ALU.mult, op1=ALU.add,
             )
 
@@ -249,35 +285,47 @@ def tile_condtransportkernel_pa_t_kernel(
                 )
                 c["cross"].append(cross)
 
-        def distances(c):
+        def distances(g, c):
             c["minus_half_d2"] = work.tile([P, TILES, NX], F32, name="minus_half_d2")
             for a in range(TILES):
+                if g >= N_CHUNKS - LAST and a >= T_CLAMP:
+                    nc.scalar.activation(
+                        out=c["minus_half_d2"][:, a, :], in_=c["cross"][a][:], func=ACT.Identity,
+                        bias=c["half_sq"][:, a : a + 1],
+                    )
+                    continue
                 nc.vector.scalar_tensor_tensor(
                     out=c["minus_half_d2"][:, a, :], in0=c["cross"][a][:],
                     scalar=c["half_sq"][:, a : a + 1], in1=train["half_sx"][:],
-                    op0=ALU.subtract, op1=ALU.min,
+                    op0=ALU.add, op1=ALU.min if a < T_CLAMP else ALU.subtract,
                 )
 
-        def flip_and_exp(c):
+        def flip_and_exp(g, c):
             k_grouped = work.tile([P, CHUNK, PACK], BF16, align_bytes=64, name="k_grouped")
             for a in range(TILES):
+                clamped = a < T_CLAMP or g >= N_CHUNKS - LAST
                 flipped = pools["psum"].tile([P, PACK, P], F32, name="bank")
                 for t in range(PACK):
                     cols = slice(t * P, (t + 1) * P)
                     nc.tensor.matmul(
                         flipped[:, t, :], lhsT=c["minus_half_d2"][:, a, cols], rhs=ident[:],
-                        is_transpose=True, start=True, stop=False,
+                        is_transpose=True, start=True, stop=not clamped,
                     )
-                    nc.tensor.matmul(
-                        flipped[:, t, :], lhsT=train["minus_half_sx"][:, cols], rhs=ident[:],
-                        is_transpose=True, start=False, stop=True,
-                    )
+                    if clamped:
+                        nc.tensor.matmul(
+                            flipped[:, t, :], lhsT=train["minus_half_sx"][:, cols], rhs=ident[:],
+                            is_transpose=True, start=False, stop=True,
+                        )
                 nc.scalar.activation(
                     out=k_grouped[:, a * P : (a + 1) * P, :],
                     in_=flipped[:].rearrange("p t r -> p r t"),
                     func=ACT.Exp, scale=1.0 / 64.0,
                 )
             c["k_grouped"] = k_grouped
+
+        def clamp(c):
+            flat = c["k_grouped"][:, T_CLAMP * P :, :].rearrange("p n t -> p (n t)")
+            nc.vector.tensor_scalar(out=flat, in0=flat, scalar1=1.0, scalar2=None, op0=ALU.min)
 
         def quantise_kernel(c):
             c["kernel"] = quantise(nc, work, c["k_grouped"], "kernel")
@@ -320,32 +368,33 @@ def tile_condtransportkernel_pa_t_kernel(
                 products(chunks[g])
             for g in at_age(step, AGE_CROSS):
                 cross_products(chunks[g])
-            for g in at_age(step, 0):
-                round_y(chunks[g])
+            for g in at_age(step, AGE_PAIR):
+                pair_queries(g, chunks[g])
+            for g in at_age(step, AGE_KERNEL):
+                clamp(chunks[g])
+            for g in at_age(step, AGE_PAIR):
+                quantise_queries(chunks[g])
             for g in at_age(step, AGE_KERNEL):
                 quantise_kernel(chunks[g])
+            for g in [step] * (step < FIRST) + [g for g in at_age(step, AGE_Y) if g >= FIRST]:
+                round_y(g, chunks[g])
+                make_y(g, chunks[g])
+            if step == 0:
+                pair_x_train()
             for g in at_age(step, AGE_PAIR):
-                pair_queries(chunks[g])
                 c = chunks[g]
-                sum_squares(
-                    c,
-                    [(2 + a, c["y_psum"][:, a, :]) for a in range(2)]
-                    + [(a, c["y_f32"][:, a, :]) for a in range(2)],
-                    "sum_y",
-                )
+                sum_squares(c, c["y_rows"], "sum_y")
                 sum_squares(c, [(a, c["xm"][:, a, :]) for a in range(TILES)], "sum_x")
                 halve_sq(c)
             for g in at_age(step, AGE_CROSS):
-                distances(chunks[g])
+                distances(g, chunks[g])
             for g in at_age(step, AGE_EXP):
-                flip_and_exp(chunks[g])
+                flip_and_exp(g, chunks[g])
             for g in at_age(step, 0):
-                keep_y(chunks[g])
+                keep_y(g, chunks[g])
                 transpose_queries(chunks[g])
             for g in at_age(step, AGE_OUT):
                 add_y_mean_and_store(g, chunks[g])
-            for g in at_age(step, AGE_PAIR):
-                quantise_queries(chunks[g])
             if step == AGE_CROSS - 1:
                 train["x"] = quantise(nc, const, train["xt_grouped"], "x_train")
                 spread_half_sx()

@@ -23,15 +23,16 @@ TILES = CHUNK // P
 N_CHUNKS = NTEST // CHUNK
 HALF = 2 * P
 AHEAD = 2
-AGE_Y = -1
-FIRST = 3
+G_KEEP = 2
+V_KEEP = 0
+GATE = True
 AGE_PAIR = 1
 AGE_CROSS = 2
 AGE_EXP = 3
 AGE_KERNEL = 4
 T_CLAMP = 2
-S_EXTRA = 1
-LAST = 1
+V_PAIR = lambda g: g > 2 and g % 2 == 1
+LAST = 0
 AGE_OUT = 5
 
 FLOPS = 2 * (NX * NX * DY + NX * DM * NTEST + NTEST * NX * DY)
@@ -191,47 +192,39 @@ def tile_condtransportkernel_pa_t_kernel(
 
         def round_y(g, c):
             c["y_bf16"] = work.tile([P, TILES, DY], BF16, name="y_bf16")
-            if g < FIRST:
+            nc.vector.tensor_tensor(
+                out=c["y_bf16"][:], in0=c["ym"][:], in1=c["yv"][:], op=ALU.add
+            )
+            if V_KEEP + G_KEEP:
+                c["y_f32"] = pools["y_f32"].tile([P, V_KEEP + G_KEEP, DY], F32, name="y_f32")
+            if V_KEEP:
                 nc.vector.tensor_tensor(
-                    out=c["y_bf16"][:], in0=c["ym"][:], in1=c["yv"][:], op=ALU.add
+                    out=c["y_f32"][:, G_KEEP:, :], in0=c["ym"][:, G_KEEP : G_KEEP + V_KEEP, :], in1=c["yv"][:, G_KEEP : G_KEEP + V_KEEP, :], op=ALU.add
                 )
-            else:
-                c["y_f32"] = pools["y_f32"].tile([P, 2, DY], F32, name="y_f32")
+            elif GATE and G_KEEP:
                 nc.vector.memset(c["y_f32"][:, 0, 0:1], 0.0)
 
         def make_y(g, c):
-            if g < FIRST:
-                return
-            for a in range(2):
+            for a in range(G_KEEP):
                 nc.gpsimd.tensor_tensor(
                     out=c["y_f32"][:, a, :], in0=c["ym"][:, a, :], in1=c["yv"][:, a, :],
                     op=ALU.add,
                 )
-            for a in range(2, 4):
-                nc.gpsimd.tensor_tensor(
-                    out=c["y_bf16"][:, a, :], in0=c["ym"][:, a, :], in1=c["yv"][:, a, :],
-                    op=ALU.add,
-                )
-            for a in range(2):
-                nc.gpsimd.tensor_scalar(
-                    out=c["y_bf16"][:, a, :], in0=c["y_f32"][:, a, :], scalar1=1.0, scalar2=0.0,
-                    op0=ALU.mult, op1=ALU.add,
-                )
 
         def keep_y(g, c):
-            c["y_rows"] = []
-            for b in ([0] if g < FIRST else []) + [1]:
+            c["y_rows"], c["y_psum_rows"] = [], []
+            kept = V_KEEP + G_KEEP
+            if kept < TILES:
                 y_psum = pools["psum"].tile([P, 2, DY], F32, name="bank")
-                for a in range(2):
-                    for name in ("ym", "yv"):
-                        nc.tensor.matmul(
-                            y_psum[:, a, :], lhsT=ident_bf16[:], rhs=c[name][:, 2 * b + a, :],
-                            start=name == "ym", stop=name == "yv",
-                        )
-                    c["y_rows"].append((2 * b + a, y_psum[:, a, :]))
-            if g >= FIRST:
-                for a in range(2):
-                    c["y_rows"].append((a, c["y_f32"][:, a, :]))
+            for a in range(kept, TILES):
+                for name in ("ym", "yv"):
+                    nc.tensor.matmul(
+                        y_psum[:, a - kept, :], lhsT=ident_bf16[:], rhs=c[name][:, a, :],
+                        start=name == "ym", stop=name == "yv",
+                    )
+                c["y_psum_rows"].append((a, y_psum[:, a - kept, :]))
+            for a in range(kept):
+                c["y_rows"].append((a, c["y_f32"][:, a, :]))
 
         def transpose_queries(c):
             xm_words = c["xm"][:].bitcast(F32)
@@ -244,13 +237,15 @@ def tile_condtransportkernel_pa_t_kernel(
             c["grouped"] = work.tile([P, CHUNK, PACK], BF16, align_bytes=64, name="grouped")
             pair_words(nc.scalar.copy, c["grouped"], 0, c["banks"][0])
             pair_words(
-                nc.scalar.copy if g < AGE_EXP - AGE_PAIR + S_EXTRA else nc.vector.tensor_copy,
+                nc.vector.tensor_copy if V_PAIR(g) else nc.scalar.copy,
                 c["grouped"], 1, c["banks"][1],
             )
 
         def sum_squares(c, sources, name):
-            squares = work.tile([P, TILES, DY], BF16, name="squares_" + name)
-            c[name] = work.tile([P, TILES], F32, name=name)
+            if name not in c:
+                c["squares_" + name] = work.tile([P, TILES, DY], BF16, name="squares_" + name)
+                c[name] = work.tile([P, TILES], F32, name=name)
+            squares = c["squares_" + name]
             for a, source in sources:
                 nc.scalar.activation(
                     out=squares[:, a, :], in_=source, func=ACT.Square,
@@ -364,37 +359,38 @@ def tile_condtransportkernel_pa_t_kernel(
         for step in range(N_CHUNKS + AGE_OUT):
             for g in at_age(step, -AHEAD):
                 chunks[g] = load_chunk(g)
+            for g in at_age(step, AGE_PAIR):
+                pair_queries(g, chunks[g])
+                sum_squares(chunks[g], chunks[g]["y_psum_rows"], "sum_y")
+            for g in at_age(step, AGE_EXP):
+                flip_and_exp(g, chunks[g])
             for g in at_age(step, AGE_OUT):
                 products(chunks[g])
             for g in at_age(step, AGE_CROSS):
                 cross_products(chunks[g])
-            for g in at_age(step, AGE_PAIR):
-                pair_queries(g, chunks[g])
             for g in at_age(step, AGE_KERNEL):
                 clamp(chunks[g])
             for g in at_age(step, AGE_PAIR):
                 quantise_queries(chunks[g])
             for g in at_age(step, AGE_KERNEL):
                 quantise_kernel(chunks[g])
-            for g in [step] * (step < FIRST) + [g for g in at_age(step, AGE_Y) if g >= FIRST]:
+            for g in at_age(step, 0):
                 round_y(g, chunks[g])
                 make_y(g, chunks[g])
             if step == 0:
                 pair_x_train()
+            for g in at_age(step, AGE_OUT):
+                add_y_mean_and_store(g, chunks[g])
+            for g in at_age(step, AGE_CROSS):
+                distances(g, chunks[g])
             for g in at_age(step, AGE_PAIR):
                 c = chunks[g]
                 sum_squares(c, c["y_rows"], "sum_y")
                 sum_squares(c, [(a, c["xm"][:, a, :]) for a in range(TILES)], "sum_x")
                 halve_sq(c)
-            for g in at_age(step, AGE_CROSS):
-                distances(g, chunks[g])
-            for g in at_age(step, AGE_EXP):
-                flip_and_exp(g, chunks[g])
             for g in at_age(step, 0):
                 keep_y(g, chunks[g])
                 transpose_queries(chunks[g])
-            for g in at_age(step, AGE_OUT):
-                add_y_mean_and_store(g, chunks[g])
             if step == AGE_CROSS - 1:
                 train["x"] = quantise(nc, const, train["xt_grouped"], "x_train")
                 spread_half_sx()

@@ -30,9 +30,18 @@ AGE_PAIR = 1
 AGE_CROSS = 2
 AGE_EXP = 3
 AGE_KERNEL = 4
-T_CLAMP = 2
-V_PAIR = lambda g: g > 2 and g % 2 == 1
-LAST = 0
+T_CLAMP = 3
+V_PAIR = lambda g: g % 3 != 1
+S_FROM = 3
+T_FIRST = 3
+ORDER = 1
+KINV = 0
+KI_FIRST = True
+V_SX = ()
+XT_SPLIT = 1
+TAIL = 2
+HALVES = True
+LAST = 1
 AGE_OUT = 5
 
 FLOPS = 2 * (NX * NX * DY + NX * DM * NTEST + NTEST * NX * DY)
@@ -97,24 +106,34 @@ def tile_condtransportkernel_pa_t_kernel(
         ident_bf16 = const.tile([P, P], BF16, name="ident_bf16")
         make_identity(nc, ident_bf16[:])
 
-        def load_chunk(g):
+        def load_chunk(g, between=None):
             rows = slice(g * CHUNK, (g + 1) * CHUNK)
             xm = pools["loads"].tile([P, TILES, DX], BF16, name="xm")
             ym = pools["y_mean"].tile([P, TILES, DY], BF16, name="ym")
             yv = pools["loads"].tile([P, TILES, DY], BF16, name="yv")
-            for tile_, source in ((ym, y_mean), (yv, y_var), (xm, x_mu)):
+            for n, (tile_, source) in enumerate(((ym, y_mean), (yv, y_var), (xm, x_mu))):
+                if between and ORDER == 2 and n == 2:
+                    between()
                 nc.sync.dma_start(
                     out=tile_[:], in_=source[rows, :].rearrange("(p a) c -> p a c", a=TILES)
                 )
+            if between and ORDER == 3:
+                between()
             return {"xm": xm, "ym": ym, "yv": yv}
 
         x_train = const.tile([P, TILES, DM], BF16, name="x_train")
-        nc.sync.dma_start(out=x_train[:], in_=X_mean.rearrange("(t p) c -> p t c", p=P))
+        def load_xt():
+            for t in range(0, TILES, TILES // XT_SPLIT):
+                ts = slice(t, t + TILES // XT_SPLIT)
+                nc.sync.dma_start(out=x_train[:, ts, :], in_=X_mean.rearrange("(t p) c -> p t c", p=P)[:, ts, :])
         chunks = {}
-        for g in range(AHEAD):
-            chunks[g] = load_chunk(g)
+        if ORDER == 1:
+            load_xt()
         k_inv = const.tile([P, TILES, NX], BF16, name="k_inv")
-        nc.sync.dma_start(out=k_inv[:], in_=kXXmean_inv.rearrange("(t p) c -> p t c", p=P))
+        for g in range(AHEAD):
+            chunks[g] = load_chunk(g, load_xt if g == 0 else None)
+            if g == KINV:
+                nc.sync.dma_start(out=k_inv[:], in_=kXXmean_inv.rearrange("(t p) c -> p t c", p=P))
         z_rows = const.tile([P, PACK, DY], BF16, name="z_rows")
         for u in range(2):
             nc.sync.dma_start(
@@ -128,10 +147,16 @@ def tile_condtransportkernel_pa_t_kernel(
             squares_x = const.tile([P, TILES, DM], BF16, name="squares_x")
             train["sx"] = const.tile([P, TILES], F32, name="sx")
             for t in range(TILES):
-                nc.scalar.activation(
-                    out=squares_x[:, t, :], in_=x_train[:, t, :], func=ACT.Square,
-                    accum_out=train["sx"][:, t : t + 1],
-                )
+                sx = train["sx"][:, t : t + 1]
+                if t in V_SX:
+                    nc.vector.scalar_tensor_tensor(
+                        out=squares_x[:, t, :], in0=x_train[:, t, :], scalar=1.0,
+                        in1=x_train[:, t, :], op0=ALU.mult, op1=ALU.mult, accum_out=sx,
+                    )
+                else:
+                    nc.scalar.activation(
+                        out=squares_x[:, t, :], in_=x_train[:, t, :], func=ACT.Square, accum_out=sx
+                    )
             x_train_words = x_train[:].bitcast(F32)
             banks = transpose_words(
                 nc, pools, ident, lambda t, u: x_train_words[:, t, u * P : (u + 1) * P]
@@ -159,15 +184,18 @@ def tile_condtransportkernel_pa_t_kernel(
         def quantise_lam_operands():
             z_grouped = const.tile([P, DY, PACK], BF16, align_bytes=64, name="z_grouped")
             nc.vector.tensor_copy(out=z_grouped[:], in_=z_rows[:].rearrange("p t d -> p d t"))
-            k_inv_words = k_inv[:].bitcast(F32)
-            banks = transpose_words(
-                nc, pools, ident, lambda t, u: k_inv_words[:, t, u * P : (u + 1) * P]
-            )
+            banks = train["ki_banks"]
             ki_grouped = work.tile([P, CHUNK, PACK], BF16, align_bytes=64, name="grouped")
             for b, planes in enumerate(banks):
                 pair_words(nc.vector.tensor_copy, ki_grouped, b, planes)
             train["z"] = quantise(nc, const, z_grouped, "z")
             train["k_inv"] = quantise(nc, const, ki_grouped, "k_inv")
+
+        def transpose_k_inv():
+            k_inv_words = k_inv[:].bitcast(F32)
+            train["ki_banks"] = transpose_words(
+                nc, pools, ident, lambda t, u: k_inv_words[:, t, u * P : (u + 1) * P]
+            )
 
         def make_lam():
             ki_codes, ki_scales = train["k_inv"]
@@ -190,21 +218,16 @@ def tile_condtransportkernel_pa_t_kernel(
                 )
             train["lam"] = quantise(nc, const, lam_grouped, "lam")
 
-        def round_y(g, c):
+        def round_y(c):
             c["y_bf16"] = work.tile([P, TILES, DY], BF16, name="y_bf16")
             nc.vector.tensor_tensor(
                 out=c["y_bf16"][:], in0=c["ym"][:], in1=c["yv"][:], op=ALU.add
             )
-            if V_KEEP + G_KEEP:
-                c["y_f32"] = pools["y_f32"].tile([P, V_KEEP + G_KEEP, DY], F32, name="y_f32")
-            if V_KEEP:
-                nc.vector.tensor_tensor(
-                    out=c["y_f32"][:, G_KEEP:, :], in0=c["ym"][:, G_KEEP : G_KEEP + V_KEEP, :], in1=c["yv"][:, G_KEEP : G_KEEP + V_KEEP, :], op=ALU.add
-                )
-            elif GATE and G_KEEP:
-                nc.vector.memset(c["y_f32"][:, 0, 0:1], 0.0)
 
         def make_y(g, c):
+            if g < T_FIRST:
+                return
+            c["y_f32"] = work.tile([P, 2, DY], F32, align_bytes=64, name="k_or_y")
             for a in range(G_KEEP):
                 nc.gpsimd.tensor_tensor(
                     out=c["y_f32"][:, a, :], in0=c["ym"][:, a, :], in1=c["yv"][:, a, :],
@@ -213,16 +236,16 @@ def tile_condtransportkernel_pa_t_kernel(
 
         def keep_y(g, c):
             c["y_rows"], c["y_psum_rows"] = [], []
-            kept = V_KEEP + G_KEEP
-            if kept < TILES:
+            kept = 0 if g < T_FIRST else G_KEEP
+            for a in range(kept, TILES, 2):
                 y_psum = pools["psum"].tile([P, 2, DY], F32, name="bank")
-            for a in range(kept, TILES):
                 for name in ("ym", "yv"):
                     nc.tensor.matmul(
-                        y_psum[:, a - kept, :], lhsT=ident_bf16[:], rhs=c[name][:, a, :],
+                        y_psum[:], lhsT=ident_bf16[:], rhs=c[name][:, a : a + 2, :],
                         start=name == "ym", stop=name == "yv",
                     )
-                c["y_psum_rows"].append((a, y_psum[:, a - kept, :]))
+                for h in range(2):
+                    c["y_psum_rows"].append((a + h, y_psum[:, h, :]))
             for a in range(kept):
                 c["y_rows"].append((a, c["y_f32"][:, a, :]))
 
@@ -283,7 +306,7 @@ def tile_condtransportkernel_pa_t_kernel(
         def distances(g, c):
             c["minus_half_d2"] = work.tile([P, TILES, NX], F32, name="minus_half_d2")
             for a in range(TILES):
-                if g >= N_CHUNKS - LAST and a >= T_CLAMP:
+                if g >= N_CHUNKS - LAST and a >= S_FROM:
                     nc.scalar.activation(
                         out=c["minus_half_d2"][:, a, :], in_=c["cross"][a][:], func=ACT.Identity,
                         bias=c["half_sq"][:, a : a + 1],
@@ -296,9 +319,9 @@ def tile_condtransportkernel_pa_t_kernel(
                 )
 
         def flip_and_exp(g, c):
-            k_grouped = work.tile([P, CHUNK, PACK], BF16, align_bytes=64, name="k_grouped")
+            k_grouped = work.tile([P, CHUNK, PACK], BF16, align_bytes=64, name="k_or_y")
             for a in range(TILES):
-                clamped = a < T_CLAMP or g >= N_CHUNKS - LAST
+                clamped = a < T_CLAMP or (g >= N_CHUNKS - LAST and a >= S_FROM)
                 flipped = pools["psum"].tile([P, PACK, P], F32, name="bank")
                 for t in range(PACK):
                     cols = slice(t * P, (t + 1) * P)
@@ -322,8 +345,14 @@ def tile_condtransportkernel_pa_t_kernel(
             flat = c["k_grouped"][:, T_CLAMP * P :, :].rearrange("p n t -> p (n t)")
             nc.vector.tensor_scalar(out=flat, in0=flat, scalar1=1.0, scalar2=None, op0=ALU.min)
 
-        def quantise_kernel(c):
-            c["kernel"] = quantise(nc, work, c["k_grouped"], "kernel")
+        def quantise_kernel(c, cols=slice(0, CHUNK)):
+            if "kernel" not in c:
+                c["kernel"] = mx_tiles(work, CHUNK, "kernel")
+            codes, scales = c["kernel"]
+            nc.vector.quantize_mx(
+                out=codes[:, cols].bitcast(FP8X4), scales=scales[:, cols],
+                in_=c["k_grouped"][:, cols, :].rearrange("p n t -> p (n t)"),
+            )
 
         def products(c):
             k_codes, k_scales = c["kernel"]
@@ -356,31 +385,47 @@ def tile_condtransportkernel_pa_t_kernel(
             return [g for g in (step - age,) if 0 <= g < N_CHUNKS]
 
         square_and_transpose_x_train()
-        for step in range(N_CHUNKS + AGE_OUT):
+        for step in range(N_CHUNKS + AGE_KERNEL + 1):
             for g in at_age(step, -AHEAD):
                 chunks[g] = load_chunk(g)
             for g in at_age(step, AGE_PAIR):
                 pair_queries(g, chunks[g])
                 sum_squares(chunks[g], chunks[g]["y_psum_rows"], "sum_y")
+            tail = step > N_CHUNKS + 2 - TAIL
+            outs = [g for g in at_age(step, AGE_OUT) if g < N_CHUNKS - 2]
+            if tail:
+                for g in outs:
+                    products(chunks[g])
             for g in at_age(step, AGE_EXP):
                 flip_and_exp(g, chunks[g])
-            for g in at_age(step, AGE_OUT):
-                products(chunks[g])
+            if not tail:
+                for g in outs:
+                    products(chunks[g])
             for g in at_age(step, AGE_CROSS):
                 cross_products(chunks[g])
+            if tail:
+                for g in outs:
+                    add_y_mean_and_store(g, chunks[g])
             for g in at_age(step, AGE_KERNEL):
+                if g == N_CHUNKS - 1 and HALVES:
+                    quantise_kernel(chunks[g], slice(0, HALF))
                 clamp(chunks[g])
             for g in at_age(step, AGE_PAIR):
                 quantise_queries(chunks[g])
-            for g in at_age(step, AGE_KERNEL):
-                quantise_kernel(chunks[g])
             for g in at_age(step, 0):
-                round_y(g, chunks[g])
+                round_y(chunks[g])
+            for g in at_age(step, AGE_KERNEL):
+                quantise_kernel(chunks[g], slice(HALF if g == N_CHUNKS - 1 and HALVES else 0, CHUNK))
+                if g >= N_CHUNKS - 2:
+                    products(chunks[g])
+                    add_y_mean_and_store(g, chunks[g])
+            for g in at_age(step, 0):
                 make_y(g, chunks[g])
             if step == 0:
                 pair_x_train()
-            for g in at_age(step, AGE_OUT):
-                add_y_mean_and_store(g, chunks[g])
+            if not tail:
+                for g in outs:
+                    add_y_mean_and_store(g, chunks[g])
             for g in at_age(step, AGE_CROSS):
                 distances(g, chunks[g])
             for g in at_age(step, AGE_PAIR):
@@ -388,9 +433,13 @@ def tile_condtransportkernel_pa_t_kernel(
                 sum_squares(c, c["y_rows"], "sum_y")
                 sum_squares(c, [(a, c["xm"][:, a, :]) for a in range(TILES)], "sum_x")
                 halve_sq(c)
+            if step == 1 and KI_FIRST:
+                transpose_k_inv()
             for g in at_age(step, 0):
                 keep_y(g, chunks[g])
                 transpose_queries(chunks[g])
+            if step == 1 and not KI_FIRST:
+                transpose_k_inv()
             if step == AGE_CROSS - 1:
                 train["x"] = quantise(nc, const, train["xt_grouped"], "x_train")
                 spread_half_sx()

@@ -30,13 +30,14 @@ AGE_PAIR = 1
 AGE_CROSS = 2
 AGE_EXP = 3
 AGE_KERNEL = 4
-T_CLAMP = 3
-V_PAIR = lambda g: g % 3 != 1
-S_FROM = 3
+T_CLAMP = 2
+V_PAIR = lambda g: g % 2 == 0
+S_FROM = 2
 T_FIRST = 3
 ORDER = 1
 KINV = 0
 KI_FIRST = True
+LATE_CLAMP = False
 V_SX = ()
 XT_SPLIT = 1
 TAIL = 2
@@ -197,11 +198,13 @@ def tile_condtransportkernel_pa_t_kernel(
                 nc, pools, ident, lambda t, u: k_inv_words[:, t, u * P : (u + 1) * P]
             )
 
-        def make_lam():
+        def make_lam(b):
             ki_codes, ki_scales = train["k_inv"]
             z_codes, z_scales = train["z"]
-            lam_grouped = const.tile([P, DY, PACK], BF16, align_bytes=64, name="lam_grouped")
-            for b in range(2):
+            if b == 0:
+                train["lam_grouped"] = const.tile([P, DY, PACK], BF16, align_bytes=64, name="lam_grouped")
+            lam_grouped = train["lam_grouped"]
+            if True:
                 lam_psum = pools["psum"].tile([P, 2, DY], F32, name="bank")
                 for t in (2 * b, 2 * b + 1):
                     nc.tensor.matmul_mx(
@@ -216,7 +219,6 @@ def tile_condtransportkernel_pa_t_kernel(
                     out=lam_grouped[:, :, 2 * b : 2 * b + 2],
                     in_=lam_psum[:].rearrange("p t d -> p d t"),
                 )
-            train["lam"] = quantise(nc, const, lam_grouped, "lam")
 
         def round_y(c):
             c["y_bf16"] = work.tile([P, TILES, DY], BF16, name="y_bf16")
@@ -403,17 +405,21 @@ def tile_condtransportkernel_pa_t_kernel(
                     products(chunks[g])
             for g in at_age(step, AGE_CROSS):
                 cross_products(chunks[g])
+            for g in at_age(step, AGE_KERNEL):
+                if g == N_CHUNKS - 1 and HALVES:
+                    quantise_kernel(chunks[g], slice(0, HALF))
+                if not LATE_CLAMP or not tail:
+                    clamp(chunks[g])
             if tail:
                 for g in outs:
                     add_y_mean_and_store(g, chunks[g])
             for g in at_age(step, AGE_KERNEL):
-                if g == N_CHUNKS - 1 and HALVES:
-                    quantise_kernel(chunks[g], slice(0, HALF))
-                clamp(chunks[g])
-            for g in at_age(step, AGE_PAIR):
-                quantise_queries(chunks[g])
+                if LATE_CLAMP and tail:
+                    clamp(chunks[g])
             for g in at_age(step, 0):
                 round_y(chunks[g])
+            for g in at_age(step, AGE_PAIR):
+                quantise_queries(chunks[g])
             for g in at_age(step, AGE_KERNEL):
                 quantise_kernel(chunks[g], slice(HALF if g == N_CHUNKS - 1 and HALVES else 0, CHUNK))
                 if g >= N_CHUNKS - 2:
@@ -426,6 +432,10 @@ def tile_condtransportkernel_pa_t_kernel(
             if not tail:
                 for g in outs:
                     add_y_mean_and_store(g, chunks[g])
+            if step == AGE_CROSS:
+                make_lam(0)
+            if step == AGE_CROSS + 1:
+                train["lam"] = quantise(nc, const, train["lam_grouped"], "lam")
             for g in at_age(step, AGE_CROSS):
                 distances(g, chunks[g])
             for g in at_age(step, AGE_PAIR):
@@ -445,4 +455,4 @@ def tile_condtransportkernel_pa_t_kernel(
                 spread_half_sx()
                 quantise_lam_operands()
             if step == AGE_CROSS:
-                make_lam()
+                make_lam(1)

@@ -30,17 +30,20 @@ AGE_PAIR = 1
 AGE_CROSS = 2
 AGE_EXP = 3
 AGE_KERNEL = 4
-T_CLAMP = 2
-V_PAIR = lambda g: g % 2 == 0
-S_FROM = 2
+T_CLAMP = 3
+V_PAIR = lambda g: g >= 3
+S_FROM = 3
 T_FIRST = 3
 ORDER = 1
 KINV = 0
 KI_FIRST = True
 LATE_CLAMP = False
+X_FIRST = False
+SX0 = False
+V_COLS = lambda g: HALF if g % 5 % 2 == 0 else 0
 V_SX = ()
 XT_SPLIT = 1
-TAIL = 2
+TAIL = 1
 HALVES = True
 LAST = 1
 AGE_OUT = 5
@@ -79,11 +82,11 @@ def transpose_words(nc, pools, ident, word_block):
     return banks
 
 
-def pair_words(copy, grouped, b, planes):
+def pair_words(copy, grouped, b, planes, cols=slice(0, HALF)):
     grouped_words = grouped[:].bitcast(F32)
     copy(
-        out=grouped_words[:, b * HALF : (b + 1) * HALF, :],
-        in_=planes[:].rearrange("p u n -> p n u"),
+        out=grouped_words[:, b * HALF + cols.start : b * HALF + cols.stop, :],
+        in_=planes[:, :, cols].rearrange("p u n -> p n u"),
     )
 
 
@@ -261,10 +264,11 @@ def tile_condtransportkernel_pa_t_kernel(
         def pair_queries(g, c):
             c["grouped"] = work.tile([P, CHUNK, PACK], BF16, align_bytes=64, name="grouped")
             pair_words(nc.scalar.copy, c["grouped"], 0, c["banks"][0])
-            pair_words(
-                nc.vector.tensor_copy if V_PAIR(g) else nc.scalar.copy,
-                c["grouped"], 1, c["banks"][1],
-            )
+            n = V_COLS(g)
+            if n > 0:
+                pair_words(nc.vector.tensor_copy, c["grouped"], 1, c["banks"][1], slice(0, n))
+            if n < HALF:
+                pair_words(nc.scalar.copy, c["grouped"], 1, c["banks"][1], slice(n, HALF))
 
         def sum_squares(c, sources, name):
             if name not in c:
@@ -325,16 +329,15 @@ def tile_condtransportkernel_pa_t_kernel(
             for a in range(TILES):
                 clamped = a < T_CLAMP or (g >= N_CHUNKS - LAST and a >= S_FROM)
                 flipped = pools["psum"].tile([P, PACK, P], F32, name="bank")
-                for t in range(PACK):
-                    cols = slice(t * P, (t + 1) * P)
-                    nc.tensor.matmul(
-                        flipped[:, t, :], lhsT=c["minus_half_d2"][:, a, cols], rhs=ident[:],
-                        is_transpose=True, start=True, stop=not clamped,
-                    )
-                    if clamped:
+                parts = [c["minus_half_d2"][:, a, :]]
+                if clamped:
+                    parts.append(train["minus_half_sx"][:])
+                for n, part in enumerate(parts):
+                    for t in range(PACK):
                         nc.tensor.matmul(
-                            flipped[:, t, :], lhsT=train["minus_half_sx"][:, cols], rhs=ident[:],
-                            is_transpose=True, start=False, stop=True,
+                            flipped[:, t, :], lhsT=part[:, t * P : (t + 1) * P], rhs=ident[:],
+                            is_transpose=True, start=n == 0 and t == 0,
+                            stop=n == len(parts) - 1 and t == PACK - 1,
                         )
                 nc.scalar.activation(
                     out=k_grouped[:, a * P : (a + 1) * P, :],
@@ -356,11 +359,11 @@ def tile_condtransportkernel_pa_t_kernel(
                 in_=c["k_grouped"][:, cols, :].rearrange("p n t -> p (n t)"),
             )
 
-        def products(c):
+        def products(c, banks=(0, 1)):
             k_codes, k_scales = c["kernel"]
             lam_codes, lam_scales = train["lam"]
-            c["products"] = []
-            for b in range(TILES // 2):
+            c.setdefault("products", [])
+            for b in banks:
                 product = pools["psum"].tile([P, 2, DY], F32, name="bank")
                 for a in (2 * b, 2 * b + 1):
                     nc.tensor.matmul_mx(
@@ -387,50 +390,43 @@ def tile_condtransportkernel_pa_t_kernel(
             return [g for g in (step - age,) if 0 <= g < N_CHUNKS]
 
         square_and_transpose_x_train()
-        for step in range(N_CHUNKS + AGE_KERNEL + 1):
+        if SX0:
+            c = chunks[0]
+            sum_squares(c, [(a, c["xm"][:, a, :]) for a in range(TILES)], "sum_x")
+        for step in range(N_CHUNKS + AGE_KERNEL - 1):
             for g in at_age(step, -AHEAD):
                 chunks[g] = load_chunk(g)
             for g in at_age(step, AGE_PAIR):
                 pair_queries(g, chunks[g])
                 sum_squares(chunks[g], chunks[g]["y_psum_rows"], "sum_y")
-            tail = step > N_CHUNKS + 2 - TAIL
-            outs = [g for g in at_age(step, AGE_OUT) if g < N_CHUNKS - 2]
+            tail = step > N_CHUNKS
             if tail:
-                for g in outs:
+                for g in at_age(step, AGE_OUT):
                     products(chunks[g])
             for g in at_age(step, AGE_EXP):
                 flip_and_exp(g, chunks[g])
             if not tail:
-                for g in outs:
+                for g in at_age(step, AGE_OUT):
                     products(chunks[g])
             for g in at_age(step, AGE_CROSS):
                 cross_products(chunks[g])
             for g in at_age(step, AGE_KERNEL):
-                if g == N_CHUNKS - 1 and HALVES:
-                    quantise_kernel(chunks[g], slice(0, HALF))
-                if not LATE_CLAMP or not tail:
-                    clamp(chunks[g])
+                clamp(chunks[g])
             if tail:
-                for g in outs:
+                for g in at_age(step, AGE_OUT):
                     add_y_mean_and_store(g, chunks[g])
-            for g in at_age(step, AGE_KERNEL):
-                if LATE_CLAMP and tail:
-                    clamp(chunks[g])
             for g in at_age(step, 0):
                 round_y(chunks[g])
             for g in at_age(step, AGE_PAIR):
                 quantise_queries(chunks[g])
             for g in at_age(step, AGE_KERNEL):
-                quantise_kernel(chunks[g], slice(HALF if g == N_CHUNKS - 1 and HALVES else 0, CHUNK))
-                if g >= N_CHUNKS - 2:
-                    products(chunks[g])
-                    add_y_mean_and_store(g, chunks[g])
+                quantise_kernel(chunks[g])
             for g in at_age(step, 0):
                 make_y(g, chunks[g])
             if step == 0:
                 pair_x_train()
             if not tail:
-                for g in outs:
+                for g in at_age(step, AGE_OUT):
                     add_y_mean_and_store(g, chunks[g])
             if step == AGE_CROSS:
                 make_lam(0)
@@ -441,13 +437,17 @@ def tile_condtransportkernel_pa_t_kernel(
             for g in at_age(step, AGE_PAIR):
                 c = chunks[g]
                 sum_squares(c, c["y_rows"], "sum_y")
-                sum_squares(c, [(a, c["xm"][:, a, :]) for a in range(TILES)], "sum_x")
+                if g > 0 or not SX0:
+                    sum_squares(c, [(a, c["xm"][:, a, :]) for a in range(TILES)], "sum_x")
                 halve_sq(c)
             if step == 1 and KI_FIRST:
                 transpose_k_inv()
             for g in at_age(step, 0):
+                if X_FIRST:
+                    transpose_queries(chunks[g])
                 keep_y(g, chunks[g])
-                transpose_queries(chunks[g])
+                if not X_FIRST:
+                    transpose_queries(chunks[g])
             if step == 1 and not KI_FIRST:
                 transpose_k_inv()
             if step == AGE_CROSS - 1:
@@ -456,3 +456,13 @@ def tile_condtransportkernel_pa_t_kernel(
                 quantise_lam_operands()
             if step == AGE_CROSS:
                 make_lam(1)
+
+        last, final = chunks[N_CHUNKS - 2], chunks[N_CHUNKS - 1]
+        products(last)
+        quantise_kernel(final, slice(0, HALF))
+        products(final, (0,))
+        add_y_mean_and_store(N_CHUNKS - 2, last)
+        clamp(final)
+        quantise_kernel(final, slice(HALF, CHUNK))
+        products(final, (1,))
+        add_y_mean_and_store(N_CHUNKS - 1, final)

@@ -40,7 +40,10 @@ KI_FIRST = True
 LATE_CLAMP = False
 X_FIRST = False
 SX0 = False
-V_COLS = lambda g: HALF if g % 5 % 2 == 0 else 0
+V_COLS = lambda g: HALF if g % 5 != 1 else 0
+AGE_Y = -1
+G_ROUND = 2
+K_BUFS = 4
 V_SX = ()
 XT_SPLIT = 1
 TAIL = 1
@@ -223,20 +226,30 @@ def tile_condtransportkernel_pa_t_kernel(
                     in_=lam_psum[:].rearrange("p t d -> p d t"),
                 )
 
-        def round_y(c):
-            c["y_bf16"] = work.tile([P, TILES, DY], BF16, name="y_bf16")
+        def round_y(g, c):
+            if g <= T_FIRST:
+                c["y_bf16"] = work.tile([P, TILES, DY], BF16, name="y_bf16")
+            tiles = slice(0 if g <= T_FIRST else G_ROUND, TILES)
             nc.vector.tensor_tensor(
-                out=c["y_bf16"][:], in0=c["ym"][:], in1=c["yv"][:], op=ALU.add
+                out=c["y_bf16"][:, tiles, :], in0=c["ym"][:, tiles, :], in1=c["yv"][:, tiles, :],
+                op=ALU.add,
             )
 
         def make_y(g, c):
             if g < T_FIRST:
                 return
-            c["y_f32"] = work.tile([P, 2, DY], F32, align_bytes=64, name="k_or_y")
+            if g > T_FIRST:
+                c["y_bf16"] = work.tile([P, TILES, DY], BF16, name="y_bf16")
+            c["y_f32"] = work.tile([P, 2, DY], F32, align_bytes=64, bufs=K_BUFS, name="k_or_y")
             for a in range(G_KEEP):
                 nc.gpsimd.tensor_tensor(
                     out=c["y_f32"][:, a, :], in0=c["ym"][:, a, :], in1=c["yv"][:, a, :],
                     op=ALU.add,
+                )
+            for a in range(G_ROUND if g > T_FIRST else 0):
+                nc.gpsimd.tensor_scalar(
+                    out=c["y_bf16"][:, a, :], in0=c["y_f32"][:, a, :], scalar1=1.0, scalar2=0.0,
+                    op0=ALU.mult, op1=ALU.add,
                 )
 
         def keep_y(g, c):
@@ -325,7 +338,7 @@ def tile_condtransportkernel_pa_t_kernel(
                 )
 
         def flip_and_exp(g, c):
-            k_grouped = work.tile([P, CHUNK, PACK], BF16, align_bytes=64, name="k_or_y")
+            k_grouped = work.tile([P, CHUNK, PACK], BF16, align_bytes=64, bufs=K_BUFS, name="k_or_y")
             for a in range(TILES):
                 clamped = a < T_CLAMP or (g >= N_CHUNKS - LAST and a >= S_FROM)
                 flipped = pools["psum"].tile([P, PACK, P], F32, name="bank")
@@ -416,12 +429,12 @@ def tile_condtransportkernel_pa_t_kernel(
                 for g in at_age(step, AGE_OUT):
                     add_y_mean_and_store(g, chunks[g])
             for g in at_age(step, 0):
-                round_y(chunks[g])
+                round_y(g, chunks[g])
             for g in at_age(step, AGE_PAIR):
                 quantise_queries(chunks[g])
             for g in at_age(step, AGE_KERNEL):
                 quantise_kernel(chunks[g])
-            for g in at_age(step, 0):
+            for g in ([T_FIRST] if step == T_FIRST else []) + [g for g in at_age(step, AGE_Y) if g > T_FIRST]:
                 make_y(g, chunks[g])
             if step == 0:
                 pair_x_train()

from contextlib import ExitStack

import concourse.mybir as mybir
from concourse.masks import make_identity

F32 = mybir.dt.float32
BF16 = mybir.dt.bfloat16
U32 = mybir.dt.uint32
U8 = mybir.dt.uint8
FP8X4 = mybir.dt.float8_e4m3fn_x4
ALU = mybir.AluOpType
ACT = mybir.ActivationFunctionType

P = 128
PACK = 4
NX = 512
NTEST = 8192
DX = 256
DY = 256
DM = DX + DY
CHUNK = 512
TILES = CHUNK // P
N_CHUNKS = NTEST // CHUNK
HALF = 2 * P
AHEAD = 2
G_KEEP = 2
V_KEEP = 0
GATE = True
AGE_PAIR = 1
AGE_CROSS = 2
AGE_EXP = 3
AGE_KERNEL = 4
T_CLAMP = 3
V_PAIR = lambda g: g >= 3
S_FROM = 3
T_FIRST = 3
ORDER = 1
KINV = 0
KI_FIRST = True
LATE_CLAMP = False
X_FIRST = False
SX0 = False
V_COLS = lambda g: HALF if g % 5 != 1 else 0
AGE_Y = -1
G_ROUND = 2
K_BUFS = 4
V_SX = ()
XT_SPLIT = 1
TAIL = 1
HALVES = True
LAST = 1
AGE_OUT = 5

FLOPS = 2 * (NX * NX * DY + NX * DM * NTEST + NTEST * NX * DY)


def mx_tiles(pool, width, name):
    codes = pool.tile([P, width], U32, align_bytes=64, name=name + "_codes")
    scales = pool.tile([P, width], U8, align_bytes=64, name=name + "_scales")
    return codes, scales


def quantise(nc, pool, grouped, name):
    codes, scales = mx_tiles(pool, grouped.shape[1], name)
    nc.vector.quantize_mx(
        out=codes[:].bitcast(FP8X4),
        scales=scales[:],
        in_=grouped[:].rearrange("p n t -> p (n t)"),
    )
    return codes, scales


def transpose_words(nc, pools, ident, word_block):
    banks = []
    for b in range(CHUNK // HALF):
        planes = pools["psum"].tile([P, 2, HALF], F32, name="bank")
        for a in range(HALF // P):
            for u in range(2):
                nc.tensor.transpose(
                    out=planes[:, u, a * P : (a + 1) * P],
                    in_=word_block(b * (HALF // P) + a, u),
                    identity=ident[:],
                )
        banks.append(planes)
    return banks


def pair_words(copy, grouped, b, planes, cols=slice(0, HALF)):
    grouped_words = grouped[:].bitcast(F32)
    copy(
        out=grouped_words[:, b * HALF + cols.start : b * HALF + cols.stop, :],
        in_=planes[:, :, cols].rearrange("p u n -> p n u"),
    )


def tile_condtransportkernel_pa_t_kernel(
    tc, x_mu, y_mean, y_var, X_mean, Z_mean, kXXmean_inv, out
):
    nc = tc.nc
    with ExitStack() as stack:
        stack.enter_context(tc.manual_schedule())
        const = stack.enter_context(tc.tile_pool(name="const", bufs=1))
        work = stack.enter_context(tc.tile_pool(name="work", bufs=3))
        pools = {
            "loads": stack.enter_context(tc.tile_pool(name="loads", bufs=AHEAD + AGE_PAIR + 2)),
            "y_mean": stack.enter_context(tc.tile_pool(name="y_mean", bufs=AHEAD + AGE_OUT + 2)),
            "y_f32": stack.enter_context(tc.tile_pool(name="y_f32", bufs=4)),
            "psum": stack.enter_context(tc.psum_pool(name="psum", bufs=8)),
        }

        ident = const.tile([P, P], F32, name="ident")
        make_identity(nc, ident[:])
        ident_bf16 = const.tile([P, P], BF16, name="ident_bf16")
        make_identity(nc, ident_bf16[:])

        def load_chunk(g, between=None):
            rows = slice(g * CHUNK, (g + 1) * CHUNK)
            xm = pools["loads"].tile([P, TILES, DX], BF16, name="xm")
            ym = pools["y_mean"].tile([P, TILES, DY], BF16, name="ym")
            yv = pools["loads"].tile([P, TILES, DY], BF16, name="yv")
            for n, (tile_, source) in enumerate(((ym, y_mean), (yv, y_var), (xm, x_mu))):
                if between and ORDER == 2 and n == 2:
                    between()
                nc.sync.dma_start(
                    out=tile_[:], in_=source[rows, :].rearrange("(p a) c -> p a c", a=TILES)
                )
            if between and ORDER == 3:
                between()
            return {"xm": xm, "ym": ym, "yv": yv}

        x_train = const.tile([P, TILES, DM], BF16, name="x_train")
        def load_xt():
            for t in range(0, TILES, TILES // XT_SPLIT):
                ts = slice(t, t + TILES // XT_SPLIT)
                nc.sync.dma_start(out=x_train[:, ts, :], in_=X_mean.rearrange("(t p) c -> p t c", p=P)[:, ts, :])
        chunks = {}
        if ORDER == 1:
            load_xt()
        k_inv = const.tile([P, TILES, NX], BF16, name="k_inv")
        for g in range(AHEAD):
            chunks[g] = load_chunk(g, load_xt if g == 0 else None)
            if g == KINV:
                nc.sync.dma_start(out=k_inv[:], in_=kXXmean_inv.rearrange("(t p) c -> p t c", p=P))
        z_rows = const.tile([P, PACK, DY], BF16, name="z_rows")
        for u in range(2):
            nc.sync.dma_start(
                out=z_rows[:, 2 * u : 2 * u + 2, :],
                in_=Z_mean[u * HALF : (u + 1) * HALF, :].rearrange("(q e) d -> q e d", e=2),
            )

        train = {}

        def square_and_transpose_x_train():
            squares_x = const.tile([P, TILES, DM], BF16, name="squares_x")
            train["sx"] = const.tile([P, TILES], F32, name="sx")
            for t in range(TILES):
                sx = train["sx"][:, t : t + 1]
                if t in V_SX:
                    nc.vector.scalar_tensor_tensor(
                        out=squares_x[:, t, :], in0=x_train[:, t, :], scalar=1.0,
                        in1=x_train[:, t, :], op0=ALU.mult, op1=ALU.mult, accum_out=sx,
                    )
                else:
                    nc.scalar.activation(
                        out=squares_x[:, t, :], in_=x_train[:, t, :], func=ACT.Square, accum_out=sx
                    )
            x_train_words = x_train[:].bitcast(F32)
            banks = transpose_words(
                nc, pools, ident, lambda t, u: x_train_words[:, t, u * P : (u + 1) * P]
            )
            train["xt_grouped"] = work.tile([P, CHUNK, PACK], BF16, align_bytes=64, name="grouped")
            train["xt_banks"] = banks

        def pair_x_train():
            for b, planes in enumerate(train["xt_banks"]):
                pair_words(nc.vector.tensor_copy, train["xt_grouped"], b, planes)

        def spread_half_sx():
            spread = pools["psum"].tile([P, NX], F32, name="bank")
            for t in range(TILES):
                nc.tensor.transpose(
                    out=spread[:, t * P : (t + 1) * P],
                    in_=train["sx"][:, t : t + 1].to_broadcast([P, P]),
                    identity=ident[:],
                )
            train["half_sx"] = const.tile([P, NX], F32, name="half_sx")
            nc.scalar.mul(out=train["half_sx"][:], in_=spread[:], mul=0.5)
            train["minus_half_sx"] = const.tile([P, NX], F32, name="minus_half_sx")
            nc.scalar.mul(out=train["minus_half_sx"][:], in_=spread[:], mul=-0.5)

        def quantise_lam_operands():
            z_grouped = const.tile([P, DY, PACK], BF16, align_bytes=64, name="z_grouped")
            nc.vector.tensor_copy(out=z_grouped[:], in_=z_rows[:].rearrange("p t d -> p d t"))
            banks = train["ki_banks"]
            ki_grouped = work.tile([P, CHUNK, PACK], BF16, align_bytes=64, name="grouped")
            for b, planes in enumerate(banks):
                pair_words(nc.vector.tensor_copy, ki_grouped, b, planes)
            train["z"] = quantise(nc, const, z_grouped, "z")
            train["k_inv"] = quantise(nc, const, ki_grouped, "k_inv")

        def transpose_k_inv():
            k_inv_words = k_inv[:].bitcast(F32)
            train["ki_banks"] = transpose_words(
                nc, pools, ident, lambda t, u: k_inv_words[:, t, u * P : (u + 1) * P]
            )

        def make_lam(b):
            ki_codes, ki_scales = train["k_inv"]
            z_codes, z_scales = train["z"]
            if b == 0:
                train["lam_grouped"] = const.tile([P, DY, PACK], BF16, align_bytes=64, name="lam_grouped")
            lam_grouped = train["lam_grouped"]
            if True:
                lam_psum = pools["psum"].tile([P, 2, DY], F32, name="bank")
                for t in (2 * b, 2 * b + 1):
                    nc.tensor.matmul_mx(
                        out=lam_psum[:, t - 2 * b, :],
                        lhsT=ki_codes[:, t * P : (t + 1) * P].bitcast(FP8X4),
                        lhsT_scale=ki_scales[:, t * P : (t + 1) * P],
                        rhs=z_codes[:].bitcast(FP8X4),
                        rhs_scale=z_scales[:],
                        start=True, stop=True,
                    )
                nc.vector.tensor_copy(
                    out=lam_grouped[:, :, 2 * b : 2 * b + 2],
                    in_=lam_psum[:].rearrange("p t d -> p d t"),
                )

        def round_y(g, c):
            if g <= T_FIRST:
                c["y_bf16"] = work.tile([P, TILES, DY], BF16, name="y_bf16")
            tiles = slice(0 if g <= T_FIRST else G_ROUND, TILES)
            nc.vector.tensor_tensor(
                out=c["y_bf16"][:, tiles, :], in0=c["ym"][:, tiles, :], in1=c["yv"][:, tiles, :],
                op=ALU.add,
            )

        def make_y(g, c):
            if g < T_FIRST:
                return
            if g > T_FIRST:
                c["y_bf16"] = work.tile([P, TILES, DY], BF16, name="y_bf16")
            c["y_f32"] = work.tile([P, 2, DY], F32, align_bytes=64, bufs=K_BUFS, name="k_or_y")
            for a in range(G_KEEP):
                nc.gpsimd.tensor_tensor(
                    out=c["y_f32"][:, a, :], in0=c["ym"][:, a, :], in1=c["yv"][:, a, :],
                    op=ALU.add,
                )
            for a in range(G_ROUND if g > T_FIRST else 0):
                nc.gpsimd.tensor_scalar(
                    out=c["y_bf16"][:, a, :], in0=c["y_f32"][:, a, :], scalar1=1.0, scalar2=0.0,
                    op0=ALU.mult, op1=ALU.add,
                )

        def keep_y(g, c):
            c["y_rows"], c["y_psum_rows"] = [], []
            kept = 0 if g < T_FIRST else G_KEEP
            for a in range(kept, TILES, 2):
                y_psum = pools["psum"].tile([P, 2, DY], F32, name="bank")
                for name in ("ym", "yv"):
                    nc.tensor.matmul(
                        y_psum[:], lhsT=ident_bf16[:], rhs=c[name][:, a : a + 2, :],
                        start=name == "ym", stop=name == "yv",
                    )
                for h in range(2):
                    c["y_psum_rows"].append((a + h, y_psum[:, h, :]))
            for a in range(kept):
                c["y_rows"].append((a, c["y_f32"][:, a, :]))

        def transpose_queries(c):
            xm_words = c["xm"][:].bitcast(F32)
            y_words = c["y_bf16"][:].bitcast(F32)
            c["banks"] = transpose_words(
                nc, pools, ident, lambda a, u: (xm_words, y_words)[u][:, a, :]
            )

        def pair_queries(g, c):
            c["grouped"] = work.tile([P, CHUNK, PACK], BF16, align_bytes=64, name="grouped")
            pair_words(nc.scalar.copy, c["grouped"], 0, c["banks"][0])
            n = V_COLS(g)
            if n > 0:
                pair_words(nc.vector.tensor_copy, c["grouped"], 1, c["banks"][1], slice(0, n))
            if n < HALF:
                pair_words(nc.scalar.copy, c["grouped"], 1, c["banks"][1], slice(n, HALF))

        def sum_squares(c, sources, name):
            if name not in c:
                c["squares_" + name] = work.tile([P, TILES, DY], BF16, name="squares_" + name)
                c[name] = work.tile([P, TILES], F32, name=name)
            squares = c["squares_" + name]
            for a, source in sources:
                nc.scalar.activation(
                    out=squares[:, a, :], in_=source, func=ACT.Square,
                    accum_out=c[name][:, a : a + 1],
                )

        def halve_sq(c):
            sq = work.tile([P, TILES], F32, name="sq")
            nc.gpsimd.tensor_tensor(out=sq[:], in0=c["sum_x"][:], in1=c["sum_y"][:], op=ALU.add)
            c["half_sq"] = work.tile([P, TILES], F32, name="half_sq")
            nc.gpsimd.tensor_scalar(
                out=c["half_sq"][:], in0=sq[:], scalar1=-0.5, scalar2=0.0,
                op0=ALU.mult, op1=ALU.add,
            )

        def quantise_queries(c):
            c["query"] = quantise(nc, work, c["grouped"], "query")

        def cross_products(c):
            q_codes, q_scales = c["query"]
            xt_codes, xt_scales = train["x"]
            c["cross"] = []
            for a in range(TILES):
                cross = pools["psum"].tile([P, NX], F32, name="bank")
                nc.tensor.matmul_mx(
                    out=cross[:],
                    lhsT=q_codes[:, a * P : (a + 1) * P].bitcast(FP8X4),
                    lhsT_scale=q_scales[:, a * P : (a + 1) * P],
                    rhs=xt_codes[:].bitcast(FP8X4),
                    rhs_scale=xt_scales[:],
                    start=True, stop=True,
                )
                c["cross"].append(cross)

        def distances(g, c):
            c["minus_half_d2"] = work.tile([P, TILES, NX], F32, name="minus_half_d2")
            for a in range(TILES):
                if g >= N_CHUNKS - LAST and a >= S_FROM:
                    nc.scalar.activation(
                        out=c["minus_half_d2"][:, a, :], in_=c["cross"][a][:], func=ACT.Identity,
                        bias=c["half_sq"][:, a : a + 1],
                    )
                    continue
                nc.vector.scalar_tensor_tensor(
                    out=c["minus_half_d2"][:, a, :], in0=c["cross"][a][:],
                    scalar=c["half_sq"][:, a : a + 1], in1=train["half_sx"][:],
                    op0=ALU.add, op1=ALU.min if a < T_CLAMP else ALU.subtract,
                )

        def flip_and_exp(g, c):
            k_grouped = work.tile([P, CHUNK, PACK], BF16, align_bytes=64, bufs=K_BUFS, name="k_or_y")
            for a in range(TILES):
                clamped = a < T_CLAMP or (g >= N_CHUNKS - LAST and a >= S_FROM)
                flipped = pools["psum"].tile([P, PACK, P], F32, name="bank")
                parts = [c["minus_half_d2"][:, a, :]]
                if clamped:
                    parts.append(train["minus_half_sx"][:])
                for n, part in enumerate(parts):
                    for t in range(PACK):
                        nc.tensor.matmul(
                            flipped[:, t, :], lhsT=part[:, t * P : (t + 1) * P], rhs=ident[:],
                            is_transpose=True, start=n == 0 and t == 0,
                            stop=n == len(parts) - 1 and t == PACK - 1,
                        )
                nc.scalar.activation(
                    out=k_grouped[:, a * P : (a + 1) * P, :],
                    in_=flipped[:].rearrange("p t r -> p r t"),
                    func=ACT.Exp, scale=1.0 / 64.0,
                )
            c["k_grouped"] = k_grouped

        def clamp(c):
            flat = c["k_grouped"][:, T_CLAMP * P :, :].rearrange("p n t -> p (n t)")
            nc.vector.tensor_scalar(out=flat, in0=flat, scalar1=1.0, scalar2=None, op0=ALU.min)

        def quantise_kernel(c, cols=slice(0, CHUNK)):
            if "kernel" not in c:
                c["kernel"] = mx_tiles(work, CHUNK, "kernel")
            codes, scales = c["kernel"]
            nc.vector.quantize_mx(
                out=codes[:, cols].bitcast(FP8X4), scales=scales[:, cols],
                in_=c["k_grouped"][:, cols, :].rearrange("p n t -> p (n t)"),
            )

        def products(c, banks=(0, 1)):
            k_codes, k_scales = c["kernel"]
            lam_codes, lam_scales = train["lam"]
            c.setdefault("products", [])
            for b in banks:
                product = pools["psum"].tile([P, 2, DY], F32, name="bank")
                for a in (2 * b, 2 * b + 1):
                    nc.tensor.matmul_mx(
                        out=product[:, a - 2 * b, :],
                        lhsT=k_codes[:, a * P : (a + 1) * P].bitcast(FP8X4),
                        lhsT_scale=k_scales[:, a * P : (a + 1) * P],
                        rhs=lam_codes[:].bitcast(FP8X4),
                        rhs_scale=lam_scales[:],
                        start=True, stop=True,
                    )
                c["products"].append(product)

        def add_y_mean_and_store(g, c):
            rows = out[g * CHUNK : (g + 1) * CHUNK, :].rearrange("(p a) d -> p a d", a=TILES)
            result = work.tile([P, TILES, DY], F32, name="result")
            for b, product in enumerate(c["products"]):
                pair = slice(2 * b, 2 * b + 2)
                nc.vector.tensor_tensor(
                    out=result[:, pair, :], in0=product[:], in1=c["ym"][:, pair, :], op=ALU.add
                )
                nc.sync.dma_start(out=rows[:, pair, :], in_=result[:, pair, :])

        def at_age(step, age):
            return [g for g in (step - age,) if 0 <= g < N_CHUNKS]

        square_and_transpose_x_train()
        if SX0:
            c = chunks[0]
            sum_squares(c, [(a, c["xm"][:, a, :]) for a in range(TILES)], "sum_x")
        for step in range(N_CHUNKS + AGE_KERNEL - 1):
            for g in at_age(step, -AHEAD):
                chunks[g] = load_chunk(g)
            for g in at_age(step, AGE_PAIR):
                pair_queries(g, chunks[g])
                sum_squares(chunks[g], chunks[g]["y_psum_rows"], "sum_y")
            tail = step > N_CHUNKS
            if tail:
                for g in at_age(step, AGE_OUT):
                    products(chunks[g])
            for g in at_age(step, AGE_EXP):
                flip_and_exp(g, chunks[g])
            if not tail:
                for g in at_age(step, AGE_OUT):
                    products(chunks[g])
            for g in at_age(step, AGE_CROSS):
                cross_products(chunks[g])
            for g in at_age(step, AGE_KERNEL):
                clamp(chunks[g])
            if tail:
                for g in at_age(step, AGE_OUT):
                    add_y_mean_and_store(g, chunks[g])
            for g in at_age(step, 0):
                round_y(g, chunks[g])
            for g in at_age(step, AGE_PAIR):
                quantise_queries(chunks[g])
            for g in at_age(step, AGE_KERNEL):
                quantise_kernel(chunks[g])
            for g in ([T_FIRST] if step == T_FIRST else []) + [g for g in at_age(step, AGE_Y) if g > T_FIRST]:
                make_y(g, chunks[g])
            if step == 0:
                pair_x_train()
            if not tail:
                for g in at_age(step, AGE_OUT):
                    add_y_mean_and_store(g, chunks[g])
            if step == AGE_CROSS:
                make_lam(0)
            if step == AGE_CROSS + 1:
                train["lam"] = quantise(nc, const, train["lam_grouped"], "lam")
            for g in at_age(step, AGE_CROSS):
                distances(g, chunks[g])
            for g in at_age(step, AGE_PAIR):
                c = chunks[g]
                sum_squares(c, c["y_rows"], "sum_y")
                if g > 0 or not SX0:
                    sum_squares(c, [(a, c["xm"][:, a, :]) for a in range(TILES)], "sum_x")
                halve_sq(c)
            if step == 1 and KI_FIRST:
                transpose_k_inv()
            for g in at_age(step, 0):
                if X_FIRST:
                    transpose_queries(chunks[g])
                keep_y(g, chunks[g])
                if not X_FIRST:
                    transpose_queries(chunks[g])
            if step == 1 and not KI_FIRST:
                transpose_k_inv()
            if step == AGE_CROSS - 1:
                train["x"] = quantise(nc, const, train["xt_grouped"], "x_train")
                spread_half_sx()
                quantise_lam_operands()
            if step == AGE_CROSS:
                make_lam(1)

        last, final = chunks[N_CHUNKS - 2], chunks[N_CHUNKS - 1]
        products(last)
        quantise_kernel(final, slice(0, HALF))
        products(final, (0,))
        add_y_mean_and_store(N_CHUNKS - 2, last)
        clamp(final)
        quantise_kernel(final, slice(HALF, CHUNK))
        products(final, (1,))
        add_y_mean_and_store(N_CHUNKS - 1, final)
